import numpy as np
import ml_dtypes


def mxq(x, axis, fmt="e4m3"):
    dtype, down = {"e4m3": (ml_dtypes.float8_e4m3fn, 7), "e5m2": (ml_dtypes.float8_e5m2, 14)}[fmt]
    v = np.moveaxis(np.asarray(x, np.float32).astype(ml_dtypes.bfloat16).astype(np.float64), axis, -1)
    blocks = v.reshape(v.shape[:-1] + (-1, 32))
    amax = np.abs(blocks).max(-1, keepdims=True)
    byte = np.maximum(np.where(amax > 0, np.frexp(amax)[1] - 1 + 127, 0) - down, 1)
    scale = np.exp2(byte - 127.0)
    codes = (blocks / scale).astype(np.float32).astype(dtype).astype(np.float64)
    return np.moveaxis((codes * scale).reshape(v.shape), -1, axis)


WIDE = False


def mx_kscale(k):
    if not WIDE:
        return np.ones(k)
    levels = np.array([10, -10, 5, -5, 0])
    if k % 512:
        return np.exp2(np.random.permutation(np.resize(levels, k // 32))).repeat(32)
    a = np.empty((k // 512, 16))
    for p in range(k // 512):
        a[p, :8] = np.random.permutation(np.resize(levels, 8))
        for g in range(8):
            far = levels[np.abs(levels - a[p, g]) >= 10]
            a[p, g + 8] = far[np.random.randint(len(far))]
    return np.exp2(a.ravel()).repeat(32)


BF16 = ml_dtypes.bfloat16


def bf(x):
    return np.asarray(x, np.float32).astype(BF16)


def f64(x):
    return np.asarray(x).astype(np.float64)


B, H, W, C, NH, WS, SH, HID = 2, 32, 16, 512, 16, 16, 7, 2048
HD = C // NH
WW = WS * WS
PT, PL = WS - SH, WS - SH
HP, WP = H + WS, W + WS
NWH, NWW = HP // WS, WP // WS
NWIN = B * NWH * NWW
EPS = 1e-5
ERF_CLIP, ERF_TERMS = 6.0, 100


def erf(z):
    z = np.clip(z, -ERF_CLIP, ERF_CLIP)
    zz = 2.0 * z * z
    term = z.copy()
    total = z.copy()
    for n in range(1, ERF_TERMS):
        term = term * zz / (2.0 * n + 1.0)
        total = total + term
    return 2.0 / np.sqrt(np.pi) * np.exp(-z * z) * total


def gelu(v):
    return 0.5 * v * (1.0 + erf(v / np.sqrt(2.0)))


def layer_norm(x, g, b):
    m = x.mean(-1, keepdims=True)
    v = ((x - m) ** 2).mean(-1, keepdims=True)
    return (x - m) / np.sqrt(v + EPS) * g + b


def setup_inputs():
    r = np.random.standard_normal
    s = mx_kscale(C)
    return {
        "h_pad": bf(r((B, HP, WP, C)) * 0.7),
        "x": bf(r((B, H * W, C))),
        "sw": bf(r((NH, WW, WW)) / np.sqrt(WW)),
        "sb": bf(r((NH, WW)) * 0.3),
        "g2": bf((1.0 + 0.2 * r(C)) * s),
        "b2": bf(0.2 * r(C) * s),
        "w1": bf(r((C, HID)) / np.sqrt(C) / s[:, None]),
        "bb1": bf(r(HID) * 0.3),
    }


def reference(h_pad, x, sw, sb, g2, b2, w1, bb1):
    hw = (f64(h_pad).reshape(B, NWH, WS, NWW, WS, NH, HD)
          .transpose(5, 2, 4, 0, 1, 3, 6)
          .reshape(NH, WW, NWIN * HD))
    m = f64(sw) @ hw + f64(sb)[:, :, None]
    m = (m.reshape(NH, WS, WS, B, NWH, NWW, HD)
          .transpose(3, 4, 1, 5, 2, 0, 6)
          .reshape(B, HP, WP, C))
    m = m[:, PT:PT + H, PL:PL + W, :].reshape(B, H * W, C)
    x1 = f64(x) + m
    h2 = layer_norm(x1, f64(g2), f64(b2))
    a = (mxq(h2, 2, "e4m3") @ mxq(f64(w1), 0, "e4m3")) + f64(bb1)
    return gelu(a)

@@ -1,0 +1,378 @@
+from contextlib import ExitStack
+
+import concourse.mybir as mybir
+from concourse.masks import make_identity
+
+BF16 = mybir.dt.bfloat16
+F32 = mybir.dt.float32
+U32 = mybir.dt.uint32
+U8 = mybir.dt.uint8
+FP8X4 = mybir.dt.float8_e4m3fn_x4
+ACT = mybir.ActivationFunctionType
+ALU = mybir.AluOpType
+
+P = 128
+BATCH = 2
+MAP_ROWS = 32
+MAP_COLS = 16
+CH = 512
+HEADS = 16
+WS = 16
+SHIFT = 7
+HID = 2048
+HEAD_CH = CH // HEADS
+POSITIONS = WS * WS
+PAD = WS - SHIFT
+WINDOWS_DOWN = (MAP_ROWS + WS) // WS
+WINDOWS_ACROSS = (MAP_COLS + WS) // WS
+EPS = 1e-5
+
+TILE_ROWS = P // MAP_COLS
+PARITIES = 2
+TILES = BATCH * MAP_ROWS // TILE_ROWS // PARITIES
+HALVES = 2
+PACK = 4
+HEADS_PER_BANK = 4
+HEAD_BANKS = HEADS // HEADS_PER_BANK
+BF16_BLOCKS_PER_BANK = 8
+N_MX = 512
+HID_CHUNKS = HID // N_MX
+STATS = 6
+LEAD = 1
+MIX_STEPS = HEAD_BANKS + LEAD
+PAIR = 2
+STORE_HALVES = 2
+HALF_HID = HID // STORE_HALVES
+CHUNKS_PER_HALF = HID_CHUNKS // STORE_HALVES
+
+FLOPS = (
+    2 * HEADS * POSITIONS * POSITIONS * BATCH * WINDOWS_DOWN * WINDOWS_ACROSS * HEAD_CH
+    + 2 * BATCH * MAP_ROWS * MAP_COLS * CH * HID
+)
+
+
+def pieces_by_window(first, count):
+    pieces = []
+    offset = 0
+    while offset < count:
+        window, inside = divmod(first + offset, WS)
+        length = min(count - offset, WS - inside)
+        pieces.append((offset, length, inside, window))
+        offset += length
+    return pieces
+
+
+def tile_swinmlpblock_pa_kernel(tc, h_pad, x, sw, sb, g2, b2, w1, bb1, out):
+    nc = tc.nc
+
+    row_pieces = [pieces_by_window(PAD + TILE_ROWS * parity, TILE_ROWS) for parity in range(PARITIES)]
+    col_pieces = pieces_by_window(PAD, MAP_COLS)
+    patches = [[(rp, cp) for rp in reversed(row_pieces[parity]) for cp in col_pieces] for parity in range(PARITIES)]
+    first, second = 1, 0
+
+    with ExitStack() as stack:
+        const = stack.enter_context(tc.tile_pool(name="const", bufs=1))
+        keep = stack.enter_context(tc.tile_pool(name="keep", bufs=1))
+        stage = stack.enter_context(tc.tile_pool(name="stage", bufs=2))
+        results = stack.enter_context(tc.tile_pool(name="results", bufs=9))
+        flip_banks = stack.enter_context(tc.psum_pool(name="flip_banks", bufs=2))
+        mix_banks = stack.enter_context(tc.psum_pool(name="mix_banks", bufs=3))
+        mx_banks = stack.enter_context(tc.psum_pool(name="mx_banks", bufs=3))
+
+        sw_rows = [keep.tile([P, HEADS, POSITIONS], BF16, name="sw_rows%d" % s) for s in range(PARITIES)]
+        sw_flipped = [
+            keep.tile([P, len(patches[s]), HEADS, P], F32, name="sw_flipped%d" % s) for s in range(PARITIES)
+        ]
+        windows = keep.tile([P, WINDOWS_DOWN, BATCH, WINDOWS_ACROSS, HALVES * CH], BF16)
+        x_tiles = [keep.tile([P, TILES, CH], BF16, name="x_tiles%d" % s) for s in range(PARITIES)]
+        x1 = [keep.tile([P, TILES, CH], F32, name="x1_%d" % s) for s in range(PARITIES)]
+        x_norm = [keep.tile([P, TILES, PACK, P], F32, name="x_norm%d" % s) for s in range(PARITIES)]
+        w1_raw = keep.tile([P, STORE_HALVES, PACK, HALF_HID], BF16)
+        w1_codes = keep.tile([P, HID], U32, align_bytes=64)
+        w1_scales = keep.tile([P, HID], U8, align_bytes=64)
+        h2_codes = keep.tile([P, PARITIES, TILES * P], U32, align_bytes=64)
+        h2_scales = keep.tile([P, PARITIES, TILES * P], U8, align_bytes=64)
+        bias_rows = const.tile([P, HID], BF16)
+
+        small_rows = const.tile([P, P], BF16)
+        sb_raw = const.tile([HEADS, POSITIONS], BF16)
+        gain_raw = const.tile([P, PACK], BF16)
+        shift_raw = const.tile([P, PACK], BF16)
+        nc.sync.dma_start(out=sb_raw[:], in_=sb)
+        nc.vector.memset(small_rows[:], 0.0)
+        nc.scalar.dma_start(out=small_rows[0 : HID // P, :], in_=bb1.rearrange("(m p) -> m p", p=P))
+        nc.scalar.dma_start(out=gain_raw[:], in_=g2.rearrange("(p t) -> p t", t=PACK))
+        nc.scalar.dma_start(out=shift_raw[:], in_=b2.rearrange("(p t) -> p t", t=PACK))
+
+        sw_by_row = sw.rearrange("h i j -> i h j")
+        window_view = h_pad.rearrange(
+            "b (wh r) (ww q e) c -> b wh ww r q (e c)", r=WS, ww=WINDOWS_ACROSS, e=HALVES
+        )
+        x_view = x.flatten_outer_dims().rearrange("(g s p) c -> s p g c", s=PARITIES, p=P)
+        w1_view = w1.rearrange("(p t) n -> p t n", t=PACK)
+        out_rows = out.flatten_outer_dims()
+
+        def load_sw_rows(parity):
+            for h0 in range(0, HEADS, HEADS_PER_BANK):
+                for offset, length, inside, window in row_pieces[parity]:
+                    nc.sync.dma_start(
+                        out=sw_rows[parity][WS * offset : WS * (offset + length), h0 : h0 + HEADS_PER_BANK, :],
+                        in_=sw_by_row[WS * inside : WS * (inside + length), h0 : h0 + HEADS_PER_BANK, :],
+                    )
+
+        def load_window_rows(rows):
+            for ww in range(WINDOWS_ACROSS):
+                for wh in rows:
+                    for b in range(BATCH):
+                        nc.sync.dma_start(out=windows[:, wh, b, ww, :], in_=window_view[b, wh, ww])
+
+        load_sw_rows(first)
+        load_window_rows((1, 2))
+        nc.sync.dma_start(out=x_tiles[first][:], in_=x_view[first])
+        load_sw_rows(second)
+        load_window_rows((0,))
+        nc.sync.dma_start(out=x_tiles[second][:], in_=x_view[second])
+        for half in range(STORE_HALVES):
+            nc.sync.dma_start(out=w1_raw[:, half, :, :], in_=w1_view[:, :, HALF_HID * half : HALF_HID * (half + 1)])
+
+        ident_bf = const.tile([P, P], BF16)
+        ident_f32 = const.tile([P, P], F32)
+        minus_half = const.tile([P, TILES], F32)
+        make_identity(nc, ident_f32[:])
+        make_identity(nc, ident_bf[:])
+        nc.gpsimd.memset(minus_half[:], -0.5)
+
+        warm = const.tile([P, 1], F32)
+        nc.scalar.activation(out=warm[:], in_=minus_half[:, 0:1], func=ACT.Gelu)
+
+        def clear_sw_flipped(parity, engine):
+            engine.memset(sw_flipped[parity][:].rearrange("q a h m -> q (a h m)"), 0.0)
+
+        sb_rows = const.tile([P, PARITIES, P], BF16)
+        nc.vector.memset(sb_rows[:], 0.0)
+        sb_grid = sb_raw[:].rearrange("h (r c) -> h r c", c=WS)
+        for parity in range(PARITIES):
+            slot_grid = sb_rows[0:HEADS, parity, :].rearrange("h (r c) -> h r c", c=MAP_COLS)
+            for (r_off, r_len, r_in, r_win), (c_off, c_len, c_in, c_win) in patches[parity]:
+                nc.scalar.copy(
+                    out=slot_grid[:, r_off : r_off + r_len, c_off : c_off + c_len],
+                    in_=sb_grid[:, r_in : r_in + r_len, c_in : c_in + c_len],
+                )
+        pick_head = const.tile([P, HEADS, TILES * HEAD_CH], BF16)
+        nc.scalar.copy(
+            out=pick_head[:], in_=ident_bf[:, 0:HEADS].unsqueeze(2).to_broadcast([P, HEADS, TILES * HEAD_CH])
+        )
+
+        clear_sw_flipped(first, nc.vector)
+        clear_sw_flipped(second, nc.gpsimd)
+
+        gain_bias = const.tile([P, 2 * PACK], F32)
+        bias_columns = const.tile([P, HID // P], BF16)
+
+        def spread_small_vectors():
+            small_flipped = mx_banks.tile([P, BF16_BLOCKS_PER_BANK, P], BF16, tag="bank")
+            nc.tensor.transpose(small_flipped[:, 0, :], small_rows[:], ident_bf[:])
+            nc.vector.tensor_copy(out=gain_bias[:, 0:PACK], in_=gain_raw[:])
+            nc.vector.tensor_copy(out=gain_bias[:, PACK : 2 * PACK], in_=shift_raw[:])
+            nc.vector.tensor_copy(out=bias_columns[:], in_=small_flipped[:, 0, 0 : HID // P])
+            for m0 in range(0, HID // P, BF16_BLOCKS_PER_BANK):
+                bank = mx_banks.tile([P, BF16_BLOCKS_PER_BANK, P], BF16, tag="bank")
+                for mm in range(BF16_BLOCKS_PER_BANK):
+                    nc.tensor.transpose(
+                        bank[:, mm, :], bias_columns[:, m0 + mm : m0 + mm + 1].to_broadcast([P, P]), ident_bf[:]
+                    )
+                nc.vector.tensor_copy(
+                    out=bias_rows[:, P * m0 : P * (m0 + BF16_BLOCKS_PER_BANK)],
+                    in_=bank[:].rearrange("p m i -> p (m i)"),
+                )
+
+        def flip_sw(parity):
+            sw_words = sw_rows[parity][:].bitcast(F32)
+            flipped_halves = sw_flipped[parity][:].bitcast(BF16)
+            for h0 in range(0, HEADS, HEADS_PER_BANK):
+                bank = flip_banks.tile([P, HEADS_PER_BANK, P], F32, tag="flip")
+                for hh in range(HEADS_PER_BANK):
+                    nc.tensor.transpose(bank[:, hh, :], sw_words[:, h0 + hh, :], ident_f32[:])
+                bank_grid = bank[:].bitcast(BF16).rearrange("q h (r ce) -> q h r ce", ce=WS * HALVES)
+                for a, ((r_off, r_len, r_in, r_win), (c_off, c_len, c_in, c_win)) in enumerate(patches[parity]):
+                    slot_grid = flipped_halves[:, a, h0 : h0 + HEADS_PER_BANK, :].rearrange(
+                        "q h (r ce) -> q h r ce", ce=MAP_COLS * HALVES
+                    )
+                    nc.scalar.copy(
+                        out=slot_grid[:, :, r_off : r_off + r_len, HALVES * c_off : HALVES * (c_off + c_len)],
+                        in_=bank_grid[:, :, r_off : r_off + r_len, HALVES * c_in : HALVES * (c_in + c_len)],
+                    )
+
+        windows_by_half = windows[:].rearrange("q wh b ww (e c) -> q wh b ww e c", e=HALVES)
+        stats = [keep.tile([P, TILES, HEAD_BANKS, STATS], F32, name="stats%d" % s) for s in range(PARITIES)]
+
+        open_banks = {}
+
+        def add_patches(parity, k, bank, which):
+            by_half = sw_flipped[parity][:].bitcast(BF16).rearrange("q a h (m e) -> q a h e m", e=HALVES)
+            last = (len(patches[parity]) - 1, HEADS_PER_BANK - 1, HALVES - 1)
+            for a in which:
+                (r_off, r_len, r_in, r_win), (c_off, c_len, c_in, c_win) = patches[parity][a]
+                for hh in range(HEADS_PER_BANK):
+                    h = HEADS_PER_BANK * k + hh
+                    for e in range(HALVES):
+                        nc.tensor.matmul(
+                            bank[:, hh, :].rearrange("p (b u d) -> p b u d", b=BATCH, d=HEAD_CH),
+                            lhsT=by_half[:, a, h, e, :],
+                            rhs=windows_by_half[
+                                :, r_win : r_win + 2, :, c_win, e, HEAD_CH * h : HEAD_CH * (h + 1)
+                            ].rearrange("q u b d -> q b u d"),
+                            start=False,
+                            stop=((a, hh, e) == last),
+                        )
+
+        def mix(parity, steps):
+            early = len(patches[parity]) // 2
+            for step in steps:
+                if step < HEAD_BANKS:
+                    bank = mix_banks.tile([P, HEADS_PER_BANK, TILES * HEAD_CH], F32)
+                    open_banks[(parity, step)] = bank
+                    nc.tensor.matmul(
+                        bank[:].rearrange("p h n -> p (h n)"),
+                        lhsT=sb_rows[:, parity, :],
+                        rhs=pick_head[:, HEADS_PER_BANK * step : HEADS_PER_BANK * (step + 1), :].rearrange(
+                            "k h n -> k (h n)"
+                        ),
+                        start=True,
+                        stop=False,
+                    )
+                    add_patches(parity, step, bank, range(0, early))
+                if step >= LEAD:
+                    k = step - LEAD
+                    bank = open_banks[(parity, k)]
+                    add_patches(parity, k, bank, range(early, len(patches[parity])))
+                    channels = slice(P * k, P * (k + 1))
+                    nc.vector.tensor_tensor(
+                        out=x1[parity][:, :, channels].rearrange("p g (h d) -> p g h d", d=HEAD_CH),
+                        in0=bank[:].rearrange("p h (g d) -> p g h d", d=HEAD_CH),
+                        in1=x_tiles[parity][:, :, channels].rearrange("p g (h d) -> p g h d", d=HEAD_CH),
+                        op=ALU.add,
+                    )
+                    for g in range(TILES):
+                        nc.vector.bn_stats(out=stats[parity][:, g, k, :], in_=x1[parity][:, g, channels])
+
+        def normalise(parity):
+            mean_var = stage.tile([P, TILES, 2], F32)
+            for g in range(TILES):
+                nc.vector.bn_aggr(out=mean_var[:, g, :], in_=stats[parity][:, g, :, :].rearrange("p k s -> p (k s)"))
+            var_eps = stage.tile([P, TILES], F32)
+            rstd = stage.tile([P, TILES], F32)
+            nc.vector.tensor_scalar_add(out=var_eps[:], in0=mean_var[:, :, 1], scalar1=EPS)
+            nc.gpsimd.tensor_tensor(out=rstd[:], in0=var_eps[:], in1=minus_half[:], op=ALU.pow)
+            for g in range(TILES):
+                nc.vector.tensor_scalar(
+                    out=x_norm[parity][:, g, :, :],
+                    in0=x1[parity][:, g, :].rearrange("s (p t) -> s t p", t=PACK),
+                    scalar1=mean_var[:, g, 0:1],
+                    scalar2=rstd[:, g : g + 1],
+                    op0=ALU.subtract,
+                    op1=ALU.mult,
+                )
+
+        def regroup(copy, dst, src):
+            copy(out=dst.rearrange("p (n i) t -> p n t i", i=4), in_=src.rearrange("p t (n i) -> p n t i", i=4))
+
+        planes = [keep.tile([P, PACK, TILES * P], BF16, name="planes%d" % s) for s in range(PARITIES)]
+
+        def flip_h2(parity, pair):
+            tokens = slice(PAIR * P * pair, PAIR * P * (pair + 1))
+            for t0 in range(0, PACK, PAIR):
+                bank = flip_banks.tile([P, PAIR, PAIR, P], F32, tag="flip")
+                for tt in range(PAIR):
+                    for gg in range(PAIR):
+                        nc.tensor.transpose(
+                            bank[:, tt, gg, :], x_norm[parity][:, PAIR * pair + gg, t0 + tt, :], ident_f32[:]
+                        )
+                for tt in range(PAIR):
+                    t = t0 + tt
+                    nc.scalar.activation(
+                        out=planes[parity][:, t, tokens],
+                        in_=bank[:, tt, :, :].rearrange("p g m -> p (g m)"),
+                        func=ACT.Identity,
+                        scale=gain_bias[:, t : t + 1],
+                        bias=gain_bias[:, PACK + t : PACK + t + 1],
+                    )
+
+        h2_words = [keep.tile([P, TILES, P, PACK], BF16, align_bytes=64, name="h2_words%d" % s) for s in range(PARITIES)]
+
+        def quantise_h2(parity, pair):
+            for g in range(PAIR * pair, PAIR * (pair + 1)):
+                regroup(nc.vector.tensor_copy, h2_words[parity][:, g, :, :], planes[parity][:, :, P * g : P * (g + 1)])
+            for g in range(PAIR * pair, PAIR * (pair + 1)):
+                tokens = slice(P * g, P * (g + 1))
+                nc.vector.quantize_mx(
+                    out=h2_codes[:, parity, tokens].bitcast(FP8X4),
+                    scales=h2_scales[:, parity, tokens],
+                    in_=h2_words[parity][:, g, :, :].rearrange("p n t -> p (n t)"),
+                )
+
+        w1_words = keep.tile([P, HID_CHUNKS, N_MX, PACK], BF16, align_bytes=64)
+
+        def regroup_w1(copy, chunks):
+            for n in chunks:
+                half, inside = divmod(n, CHUNKS_PER_HALF)
+                regroup(copy, w1_words[:, n, :, :], w1_raw[:, half, :, N_MX * inside : N_MX * (inside + 1)])
+
+        def quantise_w1():
+            for n in range(HID_CHUNKS):
+                columns = slice(N_MX * n, N_MX * (n + 1))
+                nc.vector.quantize_mx(
+                    out=w1_codes[:, columns].bitcast(FP8X4),
+                    scales=w1_scales[:, columns],
+                    in_=w1_words[:, n, :, :].rearrange("p n t -> p (n t)"),
+                )
+
+        def project(parity, g):
+            tokens = slice(P * g, P * (g + 1))
+            first_row = P * (PARITIES * g + parity)
+            for half in range(STORE_HALVES):
+                result = results.tile([P, HALF_HID], F32)
+                for inside in range(CHUNKS_PER_HALF):
+                    columns = slice(HALF_HID * half + N_MX * inside, HALF_HID * half + N_MX * (inside + 1))
+                    here = slice(N_MX * inside, N_MX * (inside + 1))
+                    bank = mx_banks.tile([P, N_MX], F32, tag="bank")
+                    nc.tensor.matmul_mx(
+                        out=bank[:],
+                        lhsT=h2_codes[:, parity, tokens].bitcast(FP8X4),
+                        lhsT_scale=h2_scales[:, parity, tokens],
+                        rhs=w1_codes[:, columns].bitcast(FP8X4),
+                        rhs_scale=w1_scales[:, columns],
+                        start=True,
+                        stop=True,
+                    )
+                    nc.vector.tensor_tensor(out=result[:, here], in0=bank[:], in1=bias_rows[:, columns], op=ALU.add)
+                    nc.scalar.activation(out=result[:, here], in_=result[:, here], func=ACT.Gelu)
+                nc.sync.dma_start(
+                    out=out_rows[first_row : first_row + P, HALF_HID * half : HALF_HID * (half + 1)], in_=result[:]
+                )
+
+        flip_sw(first)
+        mix(first, range(MIX_STEPS))
+        spread_small_vectors()
+        flip_sw(second)
+        normalise(first)
+        mix(second, range(0, MIX_STEPS // 2 + 1))
+        regroup_w1(nc.scalar.copy, range(0, HID_CHUNKS // 2))
+        flip_h2(first, 0)
+        flip_h2(first, 1)
+        regroup_w1(nc.vector.tensor_copy, range(HID_CHUNKS // 2, HID_CHUNKS))
+        quantise_w1()
+        quantise_h2(first, 0)
+        quantise_h2(first, 1)
+        mix(second, range(MIX_STEPS // 2 + 1, MIX_STEPS))
+        project(first, 0)
+        normalise(second)
+        flip_h2(second, 0)
+        project(first, 1)
+        quantise_h2(second, 0)
+        flip_h2(second, 1)
+        project(first, 2)
+        quantise_h2(second, 1)
+        project(first, 3)
+        for g in range(TILES):
+            project(second, g)

@@ -29,18 +29,17 @@ EPS = 1e-5
 
 TILE_ROWS = P // MAP_COLS
 PARITIES = 2
-TILES = BATCH * MAP_ROWS // TILE_ROWS // PARITIES
+PAIR = MAP_ROWS // TILE_ROWS // PARITIES
 HALVES = 2
 PACK = 4
-HEADS_PER_BANK = 4
-HEAD_BANKS = HEADS // HEADS_PER_BANK
+FLIP_HEADS = 4
+MIX_HEADS = 8
+MIX_BANKS = HEADS // MIX_HEADS
+BANK_CH = MIX_HEADS * HEAD_CH
 BF16_BLOCKS_PER_BANK = 8
 N_MX = 512
 HID_CHUNKS = HID // N_MX
 STATS = 6
-LEAD = 1
-MIX_STEPS = HEAD_BANKS + LEAD
-PAIR = 2
 STORE_HALVES = 2
 HALF_HID = HID // STORE_HALVES
 CHUNKS_PER_HALF = HID_CHUNKS // STORE_HALVES
@@ -69,38 +68,37 @@ def tile_swinmlpblock_pa_kernel(tc, h_pad, x, sw, sb, g2, b2, w1, bb1, out):
     col_pieces = pieces_by_window(PAD, MAP_COLS)
     patches = [[(rp, cp) for rp in reversed(row_pieces[parity]) for cp in col_pieces] for parity in range(PARITIES)]
     first, second = 1, 0
+    units = [(parity, b) for parity in (first, second) for b in range(BATCH)]
 
     with ExitStack() as stack:
         const = stack.enter_context(tc.tile_pool(name="const", bufs=1))
         keep = stack.enter_context(tc.tile_pool(name="keep", bufs=1))
         stage = stack.enter_context(tc.tile_pool(name="stage", bufs=2))
-        results = stack.enter_context(tc.tile_pool(name="results", bufs=9))
+        results = stack.enter_context(tc.tile_pool(name="results", bufs=8))
         flip_banks = stack.enter_context(tc.psum_pool(name="flip_banks", bufs=2))
-        mix_banks = stack.enter_context(tc.psum_pool(name="mix_banks", bufs=3))
-        mx_banks = stack.enter_context(tc.psum_pool(name="mx_banks", bufs=3))
+        mix_banks = stack.enter_context(tc.psum_pool(name="mix_banks", bufs=2))
+        mx_banks = stack.enter_context(tc.psum_pool(name="mx_banks", bufs=4))
 
         sw_rows = [keep.tile([P, HEADS, POSITIONS], BF16, name="sw_rows%d" % s) for s in range(PARITIES)]
-        sw_flipped = [
-            keep.tile([P, len(patches[s]), HEADS, P], F32, name="sw_flipped%d" % s) for s in range(PARITIES)
+        mixers = [
+            keep.tile([P, len(patches[s]), HALVES, HEADS, P], BF16, name="mixers%d" % s) for s in range(PARITIES)
         ]
-        windows = keep.tile([P, WINDOWS_DOWN, BATCH, WINDOWS_ACROSS, HALVES * CH], BF16)
-        x_tiles = [keep.tile([P, TILES, CH], BF16, name="x_tiles%d" % s) for s in range(PARITIES)]
-        x1 = [keep.tile([P, TILES, CH], F32, name="x1_%d" % s) for s in range(PARITIES)]
-        x_norm = [keep.tile([P, TILES, PACK, P], F32, name="x_norm%d" % s) for s in range(PARITIES)]
-        w1_raw = keep.tile([P, STORE_HALVES, PACK, HALF_HID], BF16)
+        windows = keep.tile([P, BATCH, WINDOWS_ACROSS, WINDOWS_DOWN, HALVES * CH], BF16)
+        x_tiles = [keep.tile([P, PAIR, CH], BF16, name="x_tiles%d" % i) for i in range(len(units))]
+        w1_raw = [keep.tile([P, PACK, HALF_HID], BF16, name="w1_raw%d" % i) for i in range(STORE_HALVES)]
         w1_codes = keep.tile([P, HID], U32, align_bytes=64)
         w1_scales = keep.tile([P, HID], U8, align_bytes=64)
-        h2_codes = keep.tile([P, PARITIES, TILES * P], U32, align_bytes=64)
-        h2_scales = keep.tile([P, PARITIES, TILES * P], U8, align_bytes=64)
+        h2_codes = keep.tile([P, len(units), PAIR * P], U32, align_bytes=64)
+        h2_scales = keep.tile([P, len(units), PAIR * P], U8, align_bytes=64)
         bias_rows = const.tile([P, HID], BF16)
 
-        small_rows = const.tile([P, P], BF16)
+        bias_raw = const.tile([P, P], BF16)
         sb_raw = const.tile([HEADS, POSITIONS], BF16)
         gain_raw = const.tile([P, PACK], BF16)
         shift_raw = const.tile([P, PACK], BF16)
-        nc.sync.dma_start(out=sb_raw[:], in_=sb)
-        nc.vector.memset(small_rows[:], 0.0)
-        nc.scalar.dma_start(out=small_rows[0 : HID // P, :], in_=bb1.rearrange("(m p) -> m p", p=P))
+        nc.vector.memset(bias_raw[:], 0.0)
+        nc.scalar.dma_start(out=sb_raw[:], in_=sb)
+        nc.scalar.dma_start(out=bias_raw[0 : HID // P, :], in_=bb1.rearrange("(m p) -> m p", p=P))
         nc.scalar.dma_start(out=gain_raw[:], in_=g2.rearrange("(p t) -> p t", t=PACK))
         nc.scalar.dma_start(out=shift_raw[:], in_=b2.rearrange("(p t) -> p t", t=PACK))
 
@@ -108,45 +106,52 @@ def tile_swinmlpblock_pa_kernel(tc, h_pad, x, sw, sb, g2, b2, w1, bb1, out):
         window_view = h_pad.rearrange(
             "b (wh r) (ww q e) c -> b wh ww r q (e c)", r=WS, ww=WINDOWS_ACROSS, e=HALVES
         )
-        x_view = x.flatten_outer_dims().rearrange("(g s p) c -> s p g c", s=PARITIES, p=P)
+        x_view = x.flatten_outer_dims().rearrange("(b u s p) c -> s b p u c", b=BATCH, u=PAIR, p=P)
         w1_view = w1.rearrange("(p t) n -> p t n", t=PACK)
         out_rows = out.flatten_outer_dims()
 
         def load_sw_rows(parity):
-            for h0 in range(0, HEADS, HEADS_PER_BANK):
+            for h0 in range(0, HEADS, FLIP_HEADS):
                 for offset, length, inside, window in row_pieces[parity]:
                     nc.sync.dma_start(
-                        out=sw_rows[parity][WS * offset : WS * (offset + length), h0 : h0 + HEADS_PER_BANK, :],
-                        in_=sw_by_row[WS * inside : WS * (inside + length), h0 : h0 + HEADS_PER_BANK, :],
+                        out=sw_rows[parity][WS * offset : WS * (offset + length), h0 : h0 + FLIP_HEADS, :],
+                        in_=sw_by_row[WS * inside : WS * (inside + length), h0 : h0 + FLIP_HEADS, :],
                     )
 
-        def load_window_rows(rows):
+        def load_windows(b, rows):
             for ww in range(WINDOWS_ACROSS):
                 for wh in rows:
-                    for b in range(BATCH):
-                        nc.sync.dma_start(out=windows[:, wh, b, ww, :], in_=window_view[b, wh, ww])
+                    nc.sync.dma_start(out=windows[:, b, ww, wh, :], in_=window_view[b, wh, ww])
+
+        def load_x(i):
+            parity, b = units[i]
+            nc.sync.dma_start(out=x_tiles[i][:], in_=x_view[parity, b])
+
+        def load_w1(half):
+            nc.sync.dma_start(out=w1_raw[half][:], in_=w1_view[:, :, HALF_HID * half : HALF_HID * (half + 1)])
 
         load_sw_rows(first)
-        load_window_rows((1, 2))
-        nc.sync.dma_start(out=x_tiles[first][:], in_=x_view[first])
+        load_x(0)
+        load_windows(0, (1, 2))
+        load_w1(0)
+        load_windows(1, (1, 2))
+        load_x(1)
+        load_w1(1)
         load_sw_rows(second)
-        load_window_rows((0,))
-        nc.sync.dma_start(out=x_tiles[second][:], in_=x_view[second])
-        for half in range(STORE_HALVES):
-            nc.sync.dma_start(out=w1_raw[:, half, :, :], in_=w1_view[:, :, HALF_HID * half : HALF_HID * (half + 1)])
+        load_windows(0, (0,))
+        load_x(2)
+        load_windows(1, (0,))
+        load_x(3)
 
         ident_bf = const.tile([P, P], BF16)
         ident_f32 = const.tile([P, P], F32)
-        minus_half = const.tile([P, TILES], F32)
+        minus_half = const.tile([P, PAIR], F32)
+        nc.gpsimd.memset(minus_half[:], -0.5)
         make_identity(nc, ident_f32[:])
         make_identity(nc, ident_bf[:])
-        nc.gpsimd.memset(minus_half[:], -0.5)
 
         warm = const.tile([P, 1], F32)
         nc.scalar.activation(out=warm[:], in_=minus_half[:, 0:1], func=ACT.Gelu)
-
-        def clear_sw_flipped(parity, engine):
-            engine.memset(sw_flipped[parity][:].rearrange("q a h m -> q (a h m)"), 0.0)
 
         sb_rows = const.tile([P, PARITIES, P], BF16)
         nc.vector.memset(sb_rows[:], 0.0)
@@ -158,23 +163,28 @@ def tile_swinmlpblock_pa_kernel(tc, h_pad, x, sw, sb, g2, b2, w1, bb1, out):
                     out=slot_grid[:, r_off : r_off + r_len, c_off : c_off + c_len],
                     in_=sb_grid[:, r_in : r_in + r_len, c_in : c_in + c_len],
                 )
-        pick_head = const.tile([P, HEADS, TILES * HEAD_CH], BF16)
+        pick_head = const.tile([P, HEADS, PAIR * HEAD_CH], BF16)
         nc.scalar.copy(
-            out=pick_head[:], in_=ident_bf[:, 0:HEADS].unsqueeze(2).to_broadcast([P, HEADS, TILES * HEAD_CH])
+            out=pick_head[:], in_=ident_bf[:, 0:HEADS].unsqueeze(2).to_broadcast([P, HEADS, PAIR * HEAD_CH])
         )
 
-        clear_sw_flipped(first, nc.vector)
-        clear_sw_flipped(second, nc.gpsimd)
+        def clear(engine, parity, patch):
+            engine.memset(mixers[parity][:, patch, :, :, :].rearrange("q e h m -> q (e h m)").bitcast(F32), 0.0)
+
+        clear(nc.vector, first, 0)
+        clear(nc.gpsimd, first, 1)
+        for a in range(len(patches[second])):
+            clear(nc.gpsimd, second, a)
 
         gain_bias = const.tile([P, 2 * PACK], F32)
         bias_columns = const.tile([P, HID // P], BF16)
 
         def spread_small_vectors():
-            small_flipped = mx_banks.tile([P, BF16_BLOCKS_PER_BANK, P], BF16, tag="bank")
-            nc.tensor.transpose(small_flipped[:, 0, :], small_rows[:], ident_bf[:])
             nc.vector.tensor_copy(out=gain_bias[:, 0:PACK], in_=gain_raw[:])
             nc.vector.tensor_copy(out=gain_bias[:, PACK : 2 * PACK], in_=shift_raw[:])
-            nc.vector.tensor_copy(out=bias_columns[:], in_=small_flipped[:, 0, 0 : HID // P])
+            bias_flipped = mx_banks.tile([P, BF16_BLOCKS_PER_BANK, P], BF16, tag="bank")
+            nc.tensor.transpose(bias_flipped[:, 0, :], bias_raw[:], ident_bf[:])
+            nc.vector.tensor_copy(out=bias_columns[:], in_=bias_flipped[:, 0, 0 : HID // P])
             for m0 in range(0, HID // P, BF16_BLOCKS_PER_BANK):
                 bank = mx_banks.tile([P, BF16_BLOCKS_PER_BANK, P], BF16, tag="bank")
                 for mm in range(BF16_BLOCKS_PER_BANK):
@@ -186,193 +196,279 @@ def tile_swinmlpblock_pa_kernel(tc, h_pad, x, sw, sb, g2, b2, w1, bb1, out):
                     in_=bank[:].rearrange("p m i -> p (m i)"),
                 )
 
-        def flip_sw(parity):
+        def flip_sw(parity, k, copy):
+            h0 = FLIP_HEADS * k
             sw_words = sw_rows[parity][:].bitcast(F32)
-            flipped_halves = sw_flipped[parity][:].bitcast(BF16)
-            for h0 in range(0, HEADS, HEADS_PER_BANK):
-                bank = flip_banks.tile([P, HEADS_PER_BANK, P], F32, tag="flip")
-                for hh in range(HEADS_PER_BANK):
-                    nc.tensor.transpose(bank[:, hh, :], sw_words[:, h0 + hh, :], ident_f32[:])
-                bank_grid = bank[:].bitcast(BF16).rearrange("q h (r ce) -> q h r ce", ce=WS * HALVES)
-                for a, ((r_off, r_len, r_in, r_win), (c_off, c_len, c_in, c_win)) in enumerate(patches[parity]):
-                    slot_grid = flipped_halves[:, a, h0 : h0 + HEADS_PER_BANK, :].rearrange(
-                        "q h (r ce) -> q h r ce", ce=MAP_COLS * HALVES
+            bank = flip_banks.tile([P, FLIP_HEADS, P], F32, tag="flip")
+            for hh in range(FLIP_HEADS):
+                nc.tensor.transpose(bank[:, hh, :], sw_words[:, h0 + hh, :], ident_f32[:])
+            bank_grid = bank[:].bitcast(BF16).rearrange("q h (r c e) -> q e h r c", c=WS, e=HALVES)
+            for a, ((r_off, r_len, r_in, r_win), (c_off, c_len, c_in, c_win)) in enumerate(patches[parity]):
+                for e in range(HALVES):
+                    slot_grid = mixers[parity][:, a, e, h0 : h0 + FLIP_HEADS, :].rearrange(
+                        "q h (r c) -> q h r c", c=MAP_COLS
                     )
-                    nc.scalar.copy(
-                        out=slot_grid[:, :, r_off : r_off + r_len, HALVES * c_off : HALVES * (c_off + c_len)],
-                        in_=bank_grid[:, :, r_off : r_off + r_len, HALVES * c_in : HALVES * (c_in + c_len)],
+                    copy(
+                        out=slot_grid[:, :, r_off : r_off + r_len, c_off : c_off + c_len],
+                        in_=bank_grid[:, e, :, r_off : r_off + r_len, c_in : c_in + c_len],
                     )
 
-        windows_by_half = windows[:].rearrange("q wh b ww (e c) -> q wh b ww e c", e=HALVES)
-        stats = [keep.tile([P, TILES, HEAD_BANKS, STATS], F32, name="stats%d" % s) for s in range(PARITIES)]
+        windows_by_half = windows[:].rearrange("q b ww wh (e c) -> q b ww wh e c", e=HALVES)
+        unit_banks = {}
 
-        open_banks = {}
+        def mix_open(i):
+            parity, b = units[i]
+            for k in range(MIX_BANKS):
+                bank = mix_banks.tile([P, MIX_HEADS, PAIR * HEAD_CH], F32, tag="mix")
+                unit_banks[(i, k)] = bank
+                nc.tensor.matmul(
+                    bank[:].rearrange("p h n -> p (h n)"),
+                    lhsT=sb_rows[:, parity, :],
+                    rhs=pick_head[:, MIX_HEADS * k : MIX_HEADS * (k + 1), :].rearrange("k h n -> k (h n)"),
+                    start=True,
+                    stop=False,
+                )
 
-        def add_patches(parity, k, bank, which):
-            by_half = sw_flipped[parity][:].bitcast(BF16).rearrange("q a h (m e) -> q a h e m", e=HALVES)
-            last = (len(patches[parity]) - 1, HEADS_PER_BANK - 1, HALVES - 1)
-            for a in which:
-                (r_off, r_len, r_in, r_win), (c_off, c_len, c_in, c_win) = patches[parity][a]
-                for hh in range(HEADS_PER_BANK):
-                    h = HEADS_PER_BANK * k + hh
-                    for e in range(HALVES):
-                        nc.tensor.matmul(
-                            bank[:, hh, :].rearrange("p (b u d) -> p b u d", b=BATCH, d=HEAD_CH),
-                            lhsT=by_half[:, a, h, e, :],
-                            rhs=windows_by_half[
-                                :, r_win : r_win + 2, :, c_win, e, HEAD_CH * h : HEAD_CH * (h + 1)
-                            ].rearrange("q u b d -> q b u d"),
-                            start=False,
-                            stop=((a, hh, e) == last),
-                        )
-
-        def mix(parity, steps):
-            early = len(patches[parity]) // 2
-            for step in steps:
-                if step < HEAD_BANKS:
-                    bank = mix_banks.tile([P, HEADS_PER_BANK, TILES * HEAD_CH], F32)
-                    open_banks[(parity, step)] = bank
+        def mix_patch(i, k, a):
+            parity, b = units[i]
+            bank = unit_banks[(i, k)]
+            (r_off, r_len, r_in, r_win), (c_off, c_len, c_in, c_win) = patches[parity][a]
+            last = (len(patches[parity]) - 1, MIX_HEADS - 1, HALVES - 1)
+            for hh in range(MIX_HEADS):
+                h = MIX_HEADS * k + hh
+                for e in range(HALVES):
                     nc.tensor.matmul(
-                        bank[:].rearrange("p h n -> p (h n)"),
-                        lhsT=sb_rows[:, parity, :],
-                        rhs=pick_head[:, HEADS_PER_BANK * step : HEADS_PER_BANK * (step + 1), :].rearrange(
-                            "k h n -> k (h n)"
-                        ),
-                        start=True,
-                        stop=False,
+                        bank[:, hh, :].rearrange("p (u d) -> p u d", d=HEAD_CH),
+                        lhsT=mixers[parity][:, a, e, h, :],
+                        rhs=windows_by_half[:, b, c_win, r_win : r_win + PAIR, e, HEAD_CH * h : HEAD_CH * (h + 1)],
+                        start=False,
+                        stop=((a, hh, e) == last),
                     )
-                    add_patches(parity, step, bank, range(0, early))
-                if step >= LEAD:
-                    k = step - LEAD
-                    bank = open_banks[(parity, k)]
-                    add_patches(parity, k, bank, range(early, len(patches[parity])))
-                    channels = slice(P * k, P * (k + 1))
-                    nc.vector.tensor_tensor(
-                        out=x1[parity][:, :, channels].rearrange("p g (h d) -> p g h d", d=HEAD_CH),
-                        in0=bank[:].rearrange("p h (g d) -> p g h d", d=HEAD_CH),
-                        in1=x_tiles[parity][:, :, channels].rearrange("p g (h d) -> p g h d", d=HEAD_CH),
-                        op=ALU.add,
-                    )
-                    for g in range(TILES):
-                        nc.vector.bn_stats(out=stats[parity][:, g, k, :], in_=x1[parity][:, g, channels])
 
-        def normalise(parity):
-            mean_var = stage.tile([P, TILES, 2], F32)
-            for g in range(TILES):
-                nc.vector.bn_aggr(out=mean_var[:, g, :], in_=stats[parity][:, g, :, :].rearrange("p k s -> p (k s)"))
-            var_eps = stage.tile([P, TILES], F32)
-            rstd = stage.tile([P, TILES], F32)
+        x1 = [keep.tile([P, PAIR, CH], F32, name="x1_%d" % i) for i in range(len(units))]
+
+        def add_x(i, k):
+            channels = slice(BANK_CH * k, BANK_CH * (k + 1))
+            nc.vector.tensor_tensor(
+                out=x1[i][:, :, channels].rearrange("p u (h d) -> p u h d", d=HEAD_CH),
+                in0=unit_banks[(i, k)][:].rearrange("p h (u d) -> p u h d", d=HEAD_CH),
+                in1=x_tiles[i][:, :, channels].rearrange("p u (h d) -> p u h d", d=HEAD_CH),
+                op=ALU.add,
+            )
+
+        unit_stats = {}
+
+        def statistics(i):
+            stats = stage.tile([P, PAIR, STATS], F32)
+            mean_var = stage.tile([P, PAIR, 2], F32)
+            var_eps = stage.tile([P, PAIR], F32)
+            rstd = stage.tile([P, PAIR], F32)
+            for u in range(PAIR):
+                nc.vector.bn_stats(out=stats[:, u, :], in_=x1[i][:, u, :])
+            for u in range(PAIR):
+                nc.vector.bn_aggr(out=mean_var[:, u, :], in_=stats[:, u, :])
             nc.vector.tensor_scalar_add(out=var_eps[:], in0=mean_var[:, :, 1], scalar1=EPS)
             nc.gpsimd.tensor_tensor(out=rstd[:], in0=var_eps[:], in1=minus_half[:], op=ALU.pow)
-            for g in range(TILES):
+            unit_stats[i] = (mean_var, rstd)
+
+        def normalise(i):
+            mean_var, rstd = unit_stats[i]
+            for u in range(PAIR):
                 nc.vector.tensor_scalar(
-                    out=x_norm[parity][:, g, :, :],
-                    in0=x1[parity][:, g, :].rearrange("s (p t) -> s t p", t=PACK),
-                    scalar1=mean_var[:, g, 0:1],
-                    scalar2=rstd[:, g : g + 1],
+                    out=x1[i][:, u, :],
+                    in0=x1[i][:, u, :],
+                    scalar1=mean_var[:, u, 0:1],
+                    scalar2=rstd[:, u : u + 1],
                     op0=ALU.subtract,
                     op1=ALU.mult,
                 )
 
-        def regroup(copy, dst, src):
-            copy(out=dst.rearrange("p (n i) t -> p n t i", i=4), in_=src.rearrange("p t (n i) -> p n t i", i=4))
+        planes = [keep.tile([P, PACK, PAIR * P], BF16, name="planes%d" % s) for s in range(2)]
 
-        planes = [keep.tile([P, PACK, TILES * P], BF16, name="planes%d" % s) for s in range(PARITIES)]
-
-        def flip_h2(parity, pair):
-            tokens = slice(PAIR * P * pair, PAIR * P * (pair + 1))
-            for t0 in range(0, PACK, PAIR):
-                bank = flip_banks.tile([P, PAIR, PAIR, P], F32, tag="flip")
-                for tt in range(PAIR):
-                    for gg in range(PAIR):
-                        nc.tensor.transpose(
-                            bank[:, tt, gg, :], x_norm[parity][:, PAIR * pair + gg, t0 + tt, :], ident_f32[:]
-                        )
-                for tt in range(PAIR):
+        def flip_h2(i):
+            for t0 in range(0, PACK, 2):
+                bank = flip_banks.tile([P, 2, PAIR, P], F32, tag="flip")
+                for tt in range(2):
+                    for u in range(PAIR):
+                        nc.tensor.transpose(bank[:, tt, u, :], x1[i][:, u, t0 + tt : CH : PACK], ident_f32[:])
+                for tt in range(2):
                     t = t0 + tt
                     nc.scalar.activation(
-                        out=planes[parity][:, t, tokens],
-                        in_=bank[:, tt, :, :].rearrange("p g m -> p (g m)"),
+                        out=planes[i % 2][:, t, :],
+                        in_=bank[:, tt, :, :].rearrange("p u m -> p (u m)"),
                         func=ACT.Identity,
                         scale=gain_bias[:, t : t + 1],
                         bias=gain_bias[:, PACK + t : PACK + t + 1],
                     )
 
-        h2_words = [keep.tile([P, TILES, P, PACK], BF16, align_bytes=64, name="h2_words%d" % s) for s in range(PARITIES)]
+        def regroup(copy, dst, src):
+            copy(out=dst.rearrange("p (n i) t -> p n t i", i=4), in_=src.rearrange("p t (n i) -> p n t i", i=4))
 
-        def quantise_h2(parity, pair):
-            for g in range(PAIR * pair, PAIR * (pair + 1)):
-                regroup(nc.vector.tensor_copy, h2_words[parity][:, g, :, :], planes[parity][:, :, P * g : P * (g + 1)])
-            for g in range(PAIR * pair, PAIR * (pair + 1)):
-                tokens = slice(P * g, P * (g + 1))
-                nc.vector.quantize_mx(
-                    out=h2_codes[:, parity, tokens].bitcast(FP8X4),
-                    scales=h2_scales[:, parity, tokens],
-                    in_=h2_words[parity][:, g, :, :].rearrange("p n t -> p (n t)"),
-                )
+        h2_words = [keep.tile([P, PAIR * P, PACK], BF16, align_bytes=64, name="h2_words%d" % s) for s in range(2)]
+
+        def regroup_h2(i):
+            regroup(nc.vector.tensor_copy, h2_words[i % 2][:], planes[i % 2][:])
+
+        def quantise_h2(i):
+            nc.vector.quantize_mx(
+                out=h2_codes[:, i, :].bitcast(FP8X4),
+                scales=h2_scales[:, i, :],
+                in_=h2_words[i % 2][:].rearrange("p n t -> p (n t)"),
+            )
 
         w1_words = keep.tile([P, HID_CHUNKS, N_MX, PACK], BF16, align_bytes=64)
 
-        def regroup_w1(copy, chunks):
-            for n in chunks:
-                half, inside = divmod(n, CHUNKS_PER_HALF)
-                regroup(copy, w1_words[:, n, :, :], w1_raw[:, half, :, N_MX * inside : N_MX * (inside + 1)])
+        def regroup_w1(copy, n):
+            half, inside = divmod(n, CHUNKS_PER_HALF)
+            regroup(copy, w1_words[:, n, :, :], w1_raw[half][:, :, N_MX * inside : N_MX * (inside + 1)])
 
-        def quantise_w1():
-            for n in range(HID_CHUNKS):
-                columns = slice(N_MX * n, N_MX * (n + 1))
-                nc.vector.quantize_mx(
-                    out=w1_codes[:, columns].bitcast(FP8X4),
-                    scales=w1_scales[:, columns],
-                    in_=w1_words[:, n, :, :].rearrange("p n t -> p (n t)"),
-                )
+        def quantise_w1(n):
+            columns = slice(N_MX * n, N_MX * (n + 1))
+            nc.vector.quantize_mx(
+                out=w1_codes[:, columns].bitcast(FP8X4),
+                scales=w1_scales[:, columns],
+                in_=w1_words[:, n, :, :].rearrange("p n t -> p (n t)"),
+            )
 
-        def project(parity, g):
-            tokens = slice(P * g, P * (g + 1))
-            first_row = P * (PARITIES * g + parity)
-            for half in range(STORE_HALVES):
+        products = {}
+        open_results = {}
+
+        def multiply(i, u, n):
+            tokens = slice(P * u, P * (u + 1))
+            columns = slice(N_MX * n, N_MX * (n + 1))
+            bank = mx_banks.tile([P, N_MX], F32, tag="bank")
+            products[(i, u, n)] = bank
+            nc.tensor.matmul_mx(
+                out=bank[:],
+                lhsT=h2_codes[:, i, tokens].bitcast(FP8X4),
+                lhsT_scale=h2_scales[:, i, tokens],
+                rhs=w1_codes[:, columns].bitcast(FP8X4),
+                rhs_scale=w1_scales[:, columns],
+                start=True,
+                stop=True,
+            )
+
+        def finish(i, u, n):
+            parity, b = units[i]
+            half, inside = divmod(n, CHUNKS_PER_HALF)
+            if inside == 0:
                 result = results.tile([P, HALF_HID], F32)
-                for inside in range(CHUNKS_PER_HALF):
-                    columns = slice(HALF_HID * half + N_MX * inside, HALF_HID * half + N_MX * (inside + 1))
-                    here = slice(N_MX * inside, N_MX * (inside + 1))
-                    bank = mx_banks.tile([P, N_MX], F32, tag="bank")
-                    nc.tensor.matmul_mx(
-                        out=bank[:],
-                        lhsT=h2_codes[:, parity, tokens].bitcast(FP8X4),
-                        lhsT_scale=h2_scales[:, parity, tokens],
-                        rhs=w1_codes[:, columns].bitcast(FP8X4),
-                        rhs_scale=w1_scales[:, columns],
-                        start=True,
-                        stop=True,
-                    )
-                    nc.vector.tensor_tensor(out=result[:, here], in0=bank[:], in1=bias_rows[:, columns], op=ALU.add)
-                    nc.scalar.activation(out=result[:, here], in_=result[:, here], func=ACT.Gelu)
+                open_results[(i, u, half)] = result
+            result = open_results[(i, u, half)]
+            columns = slice(N_MX * n, N_MX * (n + 1))
+            here = slice(N_MX * inside, N_MX * (inside + 1))
+            nc.vector.tensor_tensor(
+                out=result[:, here], in0=products[(i, u, n)][:], in1=bias_rows[:, columns], op=ALU.add
+            )
+            nc.scalar.activation(out=result[:, here], in_=result[:, here], func=ACT.Gelu)
+            if inside == CHUNKS_PER_HALF - 1:
+                first_row = P * (PARITIES * (PAIR * b + u) + parity)
                 nc.sync.dma_start(
                     out=out_rows[first_row : first_row + P, HALF_HID * half : HALF_HID * (half + 1)], in_=result[:]
                 )
 
-        flip_sw(first)
-        mix(first, range(MIX_STEPS))
+        def project(i, u, n):
+            multiply(i, u, n)
+            finish(i, u, n)
+
+        sc, ve = nc.scalar.copy, nc.vector.tensor_copy
+        for k in range(4):
+            flip_sw(first, k, ve if k % 2 == 0 else sc)
+        mix_open(0)
+        for a in range(2):
+            for k in range(2):
+                mix_patch(0, k, a)
         spread_small_vectors()
-        flip_sw(second)
-        normalise(first)
-        mix(second, range(0, MIX_STEPS // 2 + 1))
-        regroup_w1(nc.scalar.copy, range(0, HID_CHUNKS // 2))
-        flip_h2(first, 0)
-        flip_h2(first, 1)
-        regroup_w1(nc.vector.tensor_copy, range(HID_CHUNKS // 2, HID_CHUNKS))
-        quantise_w1()
-        quantise_h2(first, 0)
-        quantise_h2(first, 1)
-        mix(second, range(MIX_STEPS // 2 + 1, MIX_STEPS))
-        project(first, 0)
-        normalise(second)
-        flip_h2(second, 0)
-        project(first, 1)
-        quantise_h2(second, 0)
-        flip_h2(second, 1)
-        project(first, 2)
-        quantise_h2(second, 1)
-        project(first, 3)
-        for g in range(TILES):
-            project(second, g)
+        regroup_w1(sc, 0)
+        add_x(0, 0)
+        add_x(0, 1)
+        statistics(0)
+        mix_open(1)
+        for a in range(2):
+            for k in range(2):
+                mix_patch(1, k, a)
+        regroup_w1(ve, 1)
+        normalise(0)
+        flip_h2(0)
+        quantise_w1(0)
+        quantise_w1(1)
+        add_x(1, 0)
+        regroup_h2(0)
+        add_x(1, 1)
+        quantise_h2(0)
+        statistics(1)
+        multiply(0, 0, 0)
+        multiply(0, 0, 1)
+        multiply(0, 1, 0)
+        multiply(0, 1, 1)
+        finish(0, 0, 0)
+        finish(0, 0, 1)
+        normalise(1)
+        flip_h2(1)
+        finish(0, 1, 0)
+        finish(0, 1, 1)
+        regroup_w1(sc, 2)
+        regroup_w1(ve, 3)
+        regroup_h2(1)
+        quantise_w1(2)
+        quantise_h2(1)
+        quantise_w1(3)
+        multiply(0, 0, 2)
+        multiply(0, 0, 3)
+        multiply(0, 1, 2)
+        multiply(0, 1, 3)
+        flip_sw(second, 0, sc)
+        finish(0, 0, 2)
+        finish(0, 0, 3)
+        flip_sw(second, 1, sc)
+        finish(0, 1, 2)
+        finish(0, 1, 3)
+        flip_sw(second, 2, sc)
+        project(1, 0, 0)
+        flip_sw(second, 3, sc)
+        project(1, 0, 1)
+        mix_open(2)
+        for a in range(4):
+            mix_patch(2, 0, a)
+        project(1, 0, 2)
+        project(1, 0, 3)
+        for a in range(4):
+            mix_patch(2, 1, a)
+        add_x(2, 0)
+        project(1, 1, 0)
+        add_x(2, 1)
+        mix_open(3)
+        for a in range(2):
+            mix_patch(3, 0, a)
+        project(1, 1, 1)
+        statistics(2)
+        for a in range(2,4):
+            mix_patch(3, 0, a)
+        project(1, 1, 2)
+        normalise(2)
+        flip_h2(2)
+        for a in range(2):
+            mix_patch(3, 1, a)
+        project(1, 1, 3)
+        add_x(3, 0)
+        for a in range(2,4):
+            mix_patch(3, 1, a)
+        regroup_h2(2)
+        add_x(3, 1)
+        quantise_h2(2)
+        project(2, 0, 0)
+        statistics(3)
+        project(2, 0, 1)
+        project(2, 0, 2)
+        normalise(3)
+        flip_h2(3)
+        project(2, 0, 3)
+        project(2, 1, 0)
+        regroup_h2(3)
+        project(2, 1, 1)
+        quantise_h2(3)
+        project(2, 1, 2)
+        project(2, 1, 3)
+        for u in range(2):
+            for n in range(4):
+                project(3, u, n)

@@ -136,8 +136,8 @@ def tile_swinmlpblock_pa_kernel(tc, h_pad, x, sw, sb, g2, b2, w1, bb1, out):
         load_w1(0)
         load_windows(1, (1, 2))
         load_x(1)
-        load_w1(1)
         load_sw_rows(second)
+        load_w1(1)
         load_windows(0, (0,))
         load_x(2)
         load_windows(1, (0,))
@@ -179,29 +179,44 @@ def tile_swinmlpblock_pa_kernel(tc, h_pad, x, sw, sb, g2, b2, w1, bb1, out):
         gain_bias = const.tile([P, 2 * PACK], F32)
         bias_columns = const.tile([P, HID // P], BF16)
 
-        def spread_small_vectors():
-            nc.vector.tensor_copy(out=gain_bias[:, 0:PACK], in_=gain_raw[:])
-            nc.vector.tensor_copy(out=gain_bias[:, PACK : 2 * PACK], in_=shift_raw[:])
+        def flip_bias():
             bias_flipped = mx_banks.tile([P, BF16_BLOCKS_PER_BANK, P], BF16, tag="bank")
             nc.tensor.transpose(bias_flipped[:, 0, :], bias_raw[:], ident_bf[:])
             nc.vector.tensor_copy(out=bias_columns[:], in_=bias_flipped[:, 0, 0 : HID // P])
-            for m0 in range(0, HID // P, BF16_BLOCKS_PER_BANK):
-                bank = mx_banks.tile([P, BF16_BLOCKS_PER_BANK, P], BF16, tag="bank")
-                for mm in range(BF16_BLOCKS_PER_BANK):
-                    nc.tensor.transpose(
-                        bank[:, mm, :], bias_columns[:, m0 + mm : m0 + mm + 1].to_broadcast([P, P]), ident_bf[:]
-                    )
-                nc.vector.tensor_copy(
-                    out=bias_rows[:, P * m0 : P * (m0 + BF16_BLOCKS_PER_BANK)],
-                    in_=bank[:].rearrange("p m i -> p (m i)"),
+
+        bias_banks = {}
+
+        def spread_bias(half):
+            bank = mx_banks.tile([P, BF16_BLOCKS_PER_BANK, P], BF16, tag="bank")
+            bias_banks[half] = bank
+            m0 = BF16_BLOCKS_PER_BANK * half
+            for mm in range(BF16_BLOCKS_PER_BANK):
+                nc.tensor.transpose(
+                    bank[:, mm, :], bias_columns[:, m0 + mm : m0 + mm + 1].to_broadcast([P, P]), ident_bf[:]
                 )
 
-        def flip_sw(parity, k, copy):
-            h0 = FLIP_HEADS * k
+        def keep_bias(copy, half):
+            copy(
+                out=bias_rows[:, HALF_HID * half : HALF_HID * (half + 1)],
+                in_=bias_banks[half][:].rearrange("p m i -> p (m i)"),
+            )
+
+        def widen_gain():
+            nc.vector.tensor_copy(out=gain_bias[:, 0:PACK], in_=gain_raw[:])
+            nc.vector.tensor_copy(out=gain_bias[:, PACK : 2 * PACK], in_=shift_raw[:])
+
+        sw_banks = {}
+
+        def flip_sw(parity, k):
             sw_words = sw_rows[parity][:].bitcast(F32)
             bank = flip_banks.tile([P, FLIP_HEADS, P], F32, tag="flip")
+            sw_banks[(parity, k)] = bank
             for hh in range(FLIP_HEADS):
-                nc.tensor.transpose(bank[:, hh, :], sw_words[:, h0 + hh, :], ident_f32[:])
+                nc.tensor.transpose(bank[:, hh, :], sw_words[:, FLIP_HEADS * k + hh, :], ident_f32[:])
+
+        def keep_sw(parity, k, copy):
+            h0 = FLIP_HEADS * k
+            bank = sw_banks[(parity, k)]
             bank_grid = bank[:].bitcast(BF16).rearrange("q h (r c e) -> q e h r c", c=WS, e=HALVES)
             for a, ((r_off, r_len, r_in, r_win), (c_off, c_len, c_in, c_win)) in enumerate(patches[parity]):
                 for e in range(HALVES):
@@ -288,8 +303,8 @@ def tile_swinmlpblock_pa_kernel(tc, h_pad, x, sw, sb, g2, b2, w1, bb1, out):
         def flip_h2(i):
             for t0 in range(0, PACK, 2):
                 bank = flip_banks.tile([P, 2, PAIR, P], F32, tag="flip")
-                for tt in range(2):
-                    for u in range(PAIR):
+                for u in range(PAIR):
+                    for tt in range(2):
                         nc.tensor.transpose(bank[:, tt, u, :], x1[i][:, u, t0 + tt : CH : PACK], ident_f32[:])
                 for tt in range(2):
                     t = t0 + tt
@@ -371,104 +386,140 @@ def tile_swinmlpblock_pa_kernel(tc, h_pad, x, sw, sb, g2, b2, w1, bb1, out):
             multiply(i, u, n)
             finish(i, u, n)
 
-        sc, ve = nc.scalar.copy, nc.vector.tensor_copy
-        for k in range(4):
-            flip_sw(first, k, ve if k % 2 == 0 else sc)
-        mix_open(0)
-        for a in range(2):
-            for k in range(2):
-                mix_patch(0, k, a)
-        spread_small_vectors()
-        regroup_w1(sc, 0)
-        add_x(0, 0)
-        add_x(0, 1)
-        statistics(0)
-        mix_open(1)
-        for a in range(2):
-            for k in range(2):
-                mix_patch(1, k, a)
-        regroup_w1(ve, 1)
-        normalise(0)
-        flip_h2(0)
-        quantise_w1(0)
-        quantise_w1(1)
-        add_x(1, 0)
-        regroup_h2(0)
-        add_x(1, 1)
-        quantise_h2(0)
-        statistics(1)
-        multiply(0, 0, 0)
-        multiply(0, 0, 1)
-        multiply(0, 1, 0)
-        multiply(0, 1, 1)
-        finish(0, 0, 0)
-        finish(0, 0, 1)
-        normalise(1)
-        flip_h2(1)
-        finish(0, 1, 0)
-        finish(0, 1, 1)
-        regroup_w1(sc, 2)
-        regroup_w1(ve, 3)
-        regroup_h2(1)
-        quantise_w1(2)
-        quantise_h2(1)
-        quantise_w1(3)
-        multiply(0, 0, 2)
-        multiply(0, 0, 3)
-        multiply(0, 1, 2)
-        multiply(0, 1, 3)
-        flip_sw(second, 0, sc)
-        finish(0, 0, 2)
-        finish(0, 0, 3)
-        flip_sw(second, 1, sc)
-        finish(0, 1, 2)
-        finish(0, 1, 3)
-        flip_sw(second, 2, sc)
-        project(1, 0, 0)
-        flip_sw(second, 3, sc)
-        project(1, 0, 1)
-        mix_open(2)
-        for a in range(4):
-            mix_patch(2, 0, a)
-        project(1, 0, 2)
-        project(1, 0, 3)
-        for a in range(4):
-            mix_patch(2, 1, a)
-        add_x(2, 0)
-        project(1, 1, 0)
-        add_x(2, 1)
-        mix_open(3)
-        for a in range(2):
-            mix_patch(3, 0, a)
-        project(1, 1, 1)
-        statistics(2)
-        for a in range(2,4):
-            mix_patch(3, 0, a)
-        project(1, 1, 2)
-        normalise(2)
-        flip_h2(2)
-        for a in range(2):
-            mix_patch(3, 1, a)
-        project(1, 1, 3)
-        add_x(3, 0)
-        for a in range(2,4):
-            mix_patch(3, 1, a)
-        regroup_h2(2)
-        add_x(3, 1)
-        quantise_h2(2)
-        project(2, 0, 0)
-        statistics(3)
-        project(2, 0, 1)
-        project(2, 0, 2)
-        normalise(3)
-        flip_h2(3)
-        project(2, 0, 3)
-        project(2, 1, 0)
-        regroup_h2(3)
-        project(2, 1, 1)
-        quantise_h2(3)
-        project(2, 1, 2)
-        project(2, 1, 3)
-        for u in range(2):
-            for n in range(4):
-                project(3, u, n)
+        with tc.manual_schedule():
+            sc, ve = nc.scalar.copy, nc.vector.tensor_copy
+            flip_bias()
+            mix_open(0)
+            flip_sw(first, 0)
+            flip_sw(first, 1)
+            keep_sw(first, 0, ve)
+            keep_sw(first, 1, sc)
+            spread_bias(0)
+            flip_sw(first, 2)
+            keep_sw(first, 2, ve)
+            flip_sw(first, 3)
+            keep_sw(first, 3, sc)
+            spread_bias(1)
+            keep_bias(ve, 0)
+            keep_bias(ve, 1)
+            widen_gain()
+            for a in range(2):
+                for k in range(2):
+                    mix_patch(0, k, a)
+            regroup_w1(sc, 0)
+            add_x(0, 0)
+            add_x(0, 1)
+            statistics(0)
+            mix_open(1)
+            for a in range(2):
+                for k in range(2):
+                    mix_patch(1, k, a)
+            regroup_w1(ve, 1)
+            quantise_w1(0)
+            normalise(0)
+            flip_h2(0)
+            quantise_w1(1)
+            add_x(1, 0)
+            add_x(1, 1)
+            flip_sw(second, 0)
+            statistics(1)
+            keep_sw(second, 0, sc)
+            flip_sw(second, 1)
+            regroup_h2(0)
+            keep_sw(second, 1, sc)
+            quantise_h2(0)
+            multiply(0, 0, 0)
+            multiply(0, 0, 1)
+            normalise(1)
+            flip_h2(1)
+            multiply(0, 1, 0)
+            multiply(0, 1, 1)
+            flip_sw(second, 2)
+            finish(0, 0, 0)
+            keep_sw(second, 2, sc)
+            regroup_w1(ve, 3)
+            finish(0, 0, 1)
+            flip_sw(second, 3)
+            mix_open(2)
+            finish(0, 1, 0)
+            for a in range(2):
+                mix_patch(2, 0, a)
+            regroup_h2(1)
+            keep_sw(second, 3, sc)
+            finish(0, 1, 1)
+            quantise_h2(1)
+            multiply(1, 0, 0)
+            multiply(1, 0, 1)
+            multiply(1, 1, 0)
+            multiply(1, 1, 1)
+            for a in range(2,4):
+                mix_patch(2, 0, a)
+            quantise_w1(3)
+            regroup_w1(sc, 2)
+            finish(1, 0, 0)
+            finish(1, 0, 1)
+            for a in range(2):
+                mix_patch(2, 1, a)
+            add_x(2, 0)
+            finish(1, 1, 0)
+            for a in range(2,4):
+                mix_patch(2, 1, a)
+            finish(1, 1, 1)
+            quantise_w1(2)
+            add_x(2, 1)
+            multiply(0, 0, 2)
+            multiply(0, 0, 3)
+            mix_open(3)
+            for a in range(2):
+                mix_patch(3, 0, a)
+            statistics(2)
+            finish(0, 0, 2)
+            multiply(0, 1, 2)
+            multiply(0, 1, 3)
+            for a in range(2,4):
+                mix_patch(3, 0, a)
+            finish(0, 0, 3)
+            add_x(3, 0)
+            normalise(2)
+            flip_h2(2)
+            finish(0, 1, 2)
+            multiply(1, 0, 2)
+            multiply(1, 0, 3)
+            finish(0, 1, 3)
+            for a in range(2):
+                mix_patch(3, 1, a)
+            finish(1, 0, 2)
+            regroup_h2(2)
+            for a in range(2,4):
+                mix_patch(3, 1, a)
+            finish(1, 0, 3)
+            quantise_h2(2)
+            multiply(1, 1, 2)
+            multiply(1, 1, 3)
+            add_x(3, 1)
+            statistics(3)
+            finish(1, 1, 2)
+            multiply(2, 0, 0)
+            multiply(2, 0, 1)
+            finish(1, 1, 3)
+            finish(2, 0, 0)
+            normalise(3)
+            multiply(2, 0, 2)
+            multiply(2, 0, 3)
+            flip_h2(3)
+            finish(2, 0, 1)
+            multiply(2, 1, 0)
+            finish(2, 0, 2)
+            finish(2, 0, 3)
+            multiply(2, 1, 1)
+            regroup_h2(3)
+            multiply(2, 1, 2)
+            multiply(2, 1, 3)
+            finish(2, 1, 0)
+            quantise_h2(3)
+            finish(2, 1, 1)
+            finish(2, 1, 2)
+            finish(2, 1, 3)
+            for u in range(2):
+                for n in range(4):
+                    project(3, u, n)

@@ -75,9 +75,9 @@ def tile_swinmlpblock_pa_kernel(tc, h_pad, x, sw, sb, g2, b2, w1, bb1, out):
         keep = stack.enter_context(tc.tile_pool(name="keep", bufs=1))
         stage = stack.enter_context(tc.tile_pool(name="stage", bufs=2))
         results = stack.enter_context(tc.tile_pool(name="results", bufs=8))
-        flip_banks = stack.enter_context(tc.psum_pool(name="flip_banks", bufs=2))
+        flip_banks = stack.enter_context(tc.psum_pool(name="flip_banks", bufs=3))
         mix_banks = stack.enter_context(tc.psum_pool(name="mix_banks", bufs=2))
-        mx_banks = stack.enter_context(tc.psum_pool(name="mx_banks", bufs=4))
+        mx_banks = stack.enter_context(tc.psum_pool(name="mx_banks", bufs=3))
 
         sw_rows = [keep.tile([P, HEADS, POSITIONS], BF16, name="sw_rows%d" % s) for s in range(PARITIES)]
         mixers = [
@@ -131,8 +131,8 @@ def tile_swinmlpblock_pa_kernel(tc, h_pad, x, sw, sb, g2, b2, w1, bb1, out):
             nc.sync.dma_start(out=w1_raw[half][:], in_=w1_view[:, :, HALF_HID * half : HALF_HID * (half + 1)])
 
         load_sw_rows(first)
-        load_x(0)
         load_windows(0, (1, 2))
+        load_x(0)
         load_w1(0)
         load_windows(1, (1, 2))
         load_x(1)
@@ -260,14 +260,15 @@ def tile_swinmlpblock_pa_kernel(tc, h_pad, x, sw, sb, g2, b2, w1, bb1, out):
                         stop=((a, hh, e) == last),
                     )
 
-        x1 = [keep.tile([P, PAIR, CH], F32, name="x1_%d" % i) for i in range(len(units))]
+        x1 = [keep.tile([P, PAIR, PACK, P], F32, name="x1_%d" % i) for i in range(len(units))]
 
         def add_x(i, k):
             channels = slice(BANK_CH * k, BANK_CH * (k + 1))
+            columns = slice(BANK_CH // PACK * k, BANK_CH // PACK * (k + 1))
             nc.vector.tensor_tensor(
-                out=x1[i][:, :, channels].rearrange("p u (h d) -> p u h d", d=HEAD_CH),
-                in0=unit_banks[(i, k)][:].rearrange("p h (u d) -> p u h d", d=HEAD_CH),
-                in1=x_tiles[i][:, :, channels].rearrange("p u (h d) -> p u h d", d=HEAD_CH),
+                out=x1[i][:, :, :, columns].rearrange("p u t (h c) -> p u h c t", h=MIX_HEADS),
+                in0=unit_banks[(i, k)][:].rearrange("p h (u c t) -> p u h c t", u=PAIR, t=PACK),
+                in1=x_tiles[i][:, :, channels].rearrange("p u (h c t) -> p u h c t", h=MIX_HEADS, t=PACK),
                 op=ALU.add,
             )
 
@@ -279,19 +280,19 @@ def tile_swinmlpblock_pa_kernel(tc, h_pad, x, sw, sb, g2, b2, w1, bb1, out):
             var_eps = stage.tile([P, PAIR], F32)
             rstd = stage.tile([P, PAIR], F32)
             for u in range(PAIR):
-                nc.vector.bn_stats(out=stats[:, u, :], in_=x1[i][:, u, :])
+                nc.vector.bn_stats(out=stats[:, u, :], in_=x1[i][:, u, :, :].rearrange("p t c -> p (t c)"))
             for u in range(PAIR):
                 nc.vector.bn_aggr(out=mean_var[:, u, :], in_=stats[:, u, :])
             nc.vector.tensor_scalar_add(out=var_eps[:], in0=mean_var[:, :, 1], scalar1=EPS)
             nc.gpsimd.tensor_tensor(out=rstd[:], in0=var_eps[:], in1=minus_half[:], op=ALU.pow)
             unit_stats[i] = (mean_var, rstd)
 
-        def normalise(i):
+        def normalise(engine, i):
             mean_var, rstd = unit_stats[i]
             for u in range(PAIR):
-                nc.vector.tensor_scalar(
-                    out=x1[i][:, u, :],
-                    in0=x1[i][:, u, :],
+                engine.tensor_scalar(
+                    out=x1[i][:, u, :, :],
+                    in0=x1[i][:, u, :, :],
                     scalar1=mean_var[:, u, 0:1],
                     scalar2=rstd[:, u : u + 1],
                     op0=ALU.subtract,
@@ -305,7 +306,7 @@ def tile_swinmlpblock_pa_kernel(tc, h_pad, x, sw, sb, g2, b2, w1, bb1, out):
                 bank = flip_banks.tile([P, 2, PAIR, P], F32, tag="flip")
                 for u in range(PAIR):
                     for tt in range(2):
-                        nc.tensor.transpose(bank[:, tt, u, :], x1[i][:, u, t0 + tt : CH : PACK], ident_f32[:])
+                        nc.tensor.transpose(bank[:, tt, u, :], x1[i][:, u, t0 + tt, :], ident_f32[:])
                 for tt in range(2):
                     t = t0 + tt
                     nc.scalar.activation(
@@ -366,7 +367,8 @@ def tile_swinmlpblock_pa_kernel(tc, h_pad, x, sw, sb, g2, b2, w1, bb1, out):
         def finish(i, u, n):
             parity, b = units[i]
             half, inside = divmod(n, CHUNKS_PER_HALF)
-            if inside == 0:
+            complete = (i, u, half) in open_results
+            if not complete:
                 result = results.tile([P, HALF_HID], F32)
                 open_results[(i, u, half)] = result
             result = open_results[(i, u, half)]
@@ -376,8 +378,10 @@ def tile_swinmlpblock_pa_kernel(tc, h_pad, x, sw, sb, g2, b2, w1, bb1, out):
                 out=result[:, here], in0=products[(i, u, n)][:], in1=bias_rows[:, columns], op=ALU.add
             )
             nc.scalar.activation(out=result[:, here], in_=result[:, here], func=ACT.Gelu)
-            if inside == CHUNKS_PER_HALF - 1:
-                first_row = P * (PARITIES * (PAIR * b + u) + parity)
+            first_row = P * (PARITIES * (PAIR * b + u) + parity)
+            if (i, u, half) == (len(units) - 1, PAIR - 1, STORE_HALVES - 1):
+                nc.sync.dma_start(out=out_rows[first_row : first_row + P, columns], in_=result[:, here])
+            elif complete:
                 nc.sync.dma_start(
                     out=out_rows[first_row : first_row + P, HALF_HID * half : HALF_HID * (half + 1)], in_=result[:]
                 )
@@ -388,24 +392,22 @@ def tile_swinmlpblock_pa_kernel(tc, h_pad, x, sw, sb, g2, b2, w1, bb1, out):
 
         with tc.manual_schedule():
             sc, ve = nc.scalar.copy, nc.vector.tensor_copy
-            flip_bias()
-            mix_open(0)
             flip_sw(first, 0)
             flip_sw(first, 1)
             keep_sw(first, 0, ve)
             keep_sw(first, 1, sc)
-            spread_bias(0)
             flip_sw(first, 2)
             keep_sw(first, 2, ve)
             flip_sw(first, 3)
             keep_sw(first, 3, sc)
-            spread_bias(1)
-            keep_bias(ve, 0)
-            keep_bias(ve, 1)
-            widen_gain()
+            mix_open(0)
+            flip_bias()
             for a in range(2):
                 for k in range(2):
                     mix_patch(0, k, a)
+            widen_gain()
+            spread_bias(0)
+            spread_bias(1)
             regroup_w1(sc, 0)
             add_x(0, 0)
             add_x(0, 1)
@@ -414,110 +416,110 @@ def tile_swinmlpblock_pa_kernel(tc, h_pad, x, sw, sb, g2, b2, w1, bb1, out):
             for a in range(2):
                 for k in range(2):
                     mix_patch(1, k, a)
-            regroup_w1(ve, 1)
-            quantise_w1(0)
-            normalise(0)
+            keep_bias(ve, 0)
+            normalise(nc.vector, 0)
             flip_h2(0)
-            quantise_w1(1)
+            regroup_w1(ve, 1)
             add_x(1, 0)
             add_x(1, 1)
+            quantise_w1(0)
             flip_sw(second, 0)
             statistics(1)
             keep_sw(second, 0, sc)
             flip_sw(second, 1)
+            quantise_w1(1)
             regroup_h2(0)
             keep_sw(second, 1, sc)
+            mix_open(2)
+            for a in range(2):
+                mix_patch(2, 0, a)
+            keep_bias(ve, 1)
             quantise_h2(0)
+            normalise(nc.vector, 1)
             multiply(0, 0, 0)
             multiply(0, 0, 1)
-            normalise(1)
             flip_h2(1)
             multiply(0, 1, 0)
-            multiply(0, 1, 1)
-            flip_sw(second, 2)
             finish(0, 0, 0)
+            flip_sw(second, 2)
             keep_sw(second, 2, sc)
             regroup_w1(ve, 3)
-            finish(0, 0, 1)
             flip_sw(second, 3)
-            mix_open(2)
-            finish(0, 1, 0)
-            for a in range(2):
+            for a in range(2,4):
                 mix_patch(2, 0, a)
-            regroup_h2(1)
+            finish(0, 0, 1)
             keep_sw(second, 3, sc)
-            finish(0, 1, 1)
+            multiply(0, 1, 1)
+            regroup_h2(1)
+            finish(0, 1, 0)
+            quantise_w1(3)
             quantise_h2(1)
+            finish(0, 1, 1)
             multiply(1, 0, 0)
             multiply(1, 0, 1)
-            multiply(1, 1, 0)
-            multiply(1, 1, 1)
-            for a in range(2,4):
-                mix_patch(2, 0, a)
-            quantise_w1(3)
-            regroup_w1(sc, 2)
-            finish(1, 0, 0)
-            finish(1, 0, 1)
+            add_x(2, 0)
             for a in range(2):
                 mix_patch(2, 1, a)
-            add_x(2, 0)
-            finish(1, 1, 0)
+            multiply(1, 1, 0)
+            finish(1, 0, 0)
+            regroup_w1(sc, 2)
             for a in range(2,4):
                 mix_patch(2, 1, a)
-            finish(1, 1, 1)
-            quantise_w1(2)
-            add_x(2, 1)
-            multiply(0, 0, 2)
+            finish(1, 0, 1)
+            multiply(1, 1, 1)
             multiply(0, 0, 3)
+            finish(1, 1, 0)
+            add_x(2, 1)
+            finish(1, 1, 1)
             mix_open(3)
             for a in range(2):
                 mix_patch(3, 0, a)
             statistics(2)
-            finish(0, 0, 2)
-            multiply(0, 1, 2)
             multiply(0, 1, 3)
+            multiply(1, 0, 3)
+            finish(0, 0, 3)
             for a in range(2,4):
                 mix_patch(3, 0, a)
-            finish(0, 0, 3)
-            add_x(3, 0)
-            normalise(2)
-            flip_h2(2)
-            finish(0, 1, 2)
-            multiply(1, 0, 2)
-            multiply(1, 0, 3)
             finish(0, 1, 3)
-            for a in range(2):
-                mix_patch(3, 1, a)
-            finish(1, 0, 2)
-            regroup_h2(2)
-            for a in range(2,4):
-                mix_patch(3, 1, a)
+            quantise_w1(2)
+            normalise(nc.vector, 2)
+            multiply(0, 0, 2)
+            multiply(0, 1, 2)
+            flip_h2(2)
             finish(1, 0, 3)
-            quantise_h2(2)
+            add_x(3, 0)
+            multiply(1, 0, 2)
+            for a in range(4):
+                mix_patch(3, 1, a)
+            finish(0, 0, 2)
+            finish(0, 1, 2)
             multiply(1, 1, 2)
             multiply(1, 1, 3)
+            regroup_h2(2)
+            finish(1, 0, 2)
+            quantise_h2(2)
             add_x(3, 1)
             statistics(3)
-            finish(1, 1, 2)
             multiply(2, 0, 0)
+            finish(1, 1, 2)
             multiply(2, 0, 1)
             finish(1, 1, 3)
-            finish(2, 0, 0)
-            normalise(3)
             multiply(2, 0, 2)
-            multiply(2, 0, 3)
+            finish(2, 0, 0)
+            normalise(nc.vector, 3)
             flip_h2(3)
             finish(2, 0, 1)
+            multiply(2, 0, 3)
             multiply(2, 1, 0)
             finish(2, 0, 2)
-            finish(2, 0, 3)
             multiply(2, 1, 1)
-            regroup_h2(3)
+            finish(2, 0, 3)
             multiply(2, 1, 2)
-            multiply(2, 1, 3)
             finish(2, 1, 0)
-            quantise_h2(3)
+            regroup_h2(3)
+            multiply(2, 1, 3)
             finish(2, 1, 1)
+            quantise_h2(3)
             finish(2, 1, 2)
             finish(2, 1, 3)
             for u in range(2):

@@ -103,6 +103,10 @@ def tile_swinmlpblock_pa_kernel(tc, h_pad, x, sw, sb, g2, b2, w1, bb1, out):
         nc.scalar.dma_start(out=shift_raw[:], in_=b2.rearrange("(p t) -> p t", t=PACK))
 
         sw_by_row = sw.rearrange("h i j -> i h j")
+        sw_start = WS * row_pieces[second][0][2]
+        sw_shifted = sw.flatten_outer_dims()[sw_start : sw_start + POSITIONS * (HEADS - 1), :].rearrange(
+            "(h i) j -> i h j", i=POSITIONS
+        )
         window_view = h_pad.rearrange(
             "b (wh r) (ww q e) c -> b wh ww r q (e c)", r=WS, ww=WINDOWS_ACROSS, e=HALVES
         )
@@ -111,12 +115,21 @@ def tile_swinmlpblock_pa_kernel(tc, h_pad, x, sw, sb, g2, b2, w1, bb1, out):
         out_rows = out.flatten_outer_dims()
 
         def load_sw_rows(parity):
-            for h0 in range(0, HEADS, FLIP_HEADS):
-                for offset, length, inside, window in row_pieces[parity]:
-                    nc.sync.dma_start(
-                        out=sw_rows[parity][WS * offset : WS * (offset + length), h0 : h0 + FLIP_HEADS, :],
-                        in_=sw_by_row[WS * inside : WS * (inside + length), h0 : h0 + FLIP_HEADS, :],
-                    )
+            (offset, length, inside, window), wrapped = row_pieces[parity][0], row_pieces[parity][1:]
+            split = WS * length
+            if wrapped:
+                nc.sync.dma_start(out=sw_rows[parity][0:split, 0, :], in_=sw[HEADS - 1, POSITIONS - split : POSITIONS, :])
+                nc.sync.dma_start(out=sw_rows[parity][split:P, 0, :], in_=sw[0, 0 : P - split, :])
+            for g0 in range(0, HEADS, FLIP_HEADS):
+                first_place = max(g0, len(wrapped))
+                places = slice(first_place, g0 + FLIP_HEADS)
+                heads = slice(first_place - len(wrapped), g0 + FLIP_HEADS - len(wrapped))
+                nc.sync.dma_start(
+                    out=sw_rows[parity][:, places, :],
+                    in_=sw_by_row[WS * inside : WS * inside + P, heads, :]
+                    if not wrapped
+                    else sw_shifted[0:P, heads, :],
+                )
 
         def load_windows(b, rows):
             for ww in range(WINDOWS_ACROSS):
@@ -173,7 +186,7 @@ def tile_swinmlpblock_pa_kernel(tc, h_pad, x, sw, sb, g2, b2, w1, bb1, out):
 
         clear(nc.vector, first, 0)
         clear(nc.gpsimd, first, 1)
-        for a in range(len(patches[second])):
+        for a in range(2):
             clear(nc.gpsimd, second, a)
 
         gain_bias = const.tile([P, 2 * PACK], F32)
@@ -215,18 +228,25 @@ def tile_swinmlpblock_pa_kernel(tc, h_pad, x, sw, sb, g2, b2, w1, bb1, out):
                 nc.tensor.transpose(bank[:, hh, :], sw_words[:, FLIP_HEADS * k + hh, :], ident_f32[:])
 
         def keep_sw(parity, k, copy):
-            h0 = FLIP_HEADS * k
+            g0 = FLIP_HEADS * k
             bank = sw_banks[(parity, k)]
             bank_grid = bank[:].bitcast(BF16).rearrange("q h (r c e) -> q e h r c", c=WS, e=HALVES)
             for a, ((r_off, r_len, r_in, r_win), (c_off, c_len, c_in, c_win)) in enumerate(patches[parity]):
-                for e in range(HALVES):
-                    slot_grid = mixers[parity][:, a, e, h0 : h0 + FLIP_HEADS, :].rearrange(
-                        "q h (r c) -> q h r c", c=MAP_COLS
-                    )
-                    copy(
-                        out=slot_grid[:, :, r_off : r_off + r_len, c_off : c_off + c_len],
-                        in_=bank_grid[:, e, :, r_off : r_off + r_len, c_in : c_in + c_len],
-                    )
+                if len(row_pieces[parity]) == 1 or r_off > 0:
+                    runs = [(0, FLIP_HEADS, g0)]
+                elif g0 == 0:
+                    runs = [(0, 1, HEADS - 1), (1, FLIP_HEADS - 1, 0)]
+                else:
+                    runs = [(0, FLIP_HEADS, g0 - 1)]
+                for place, count, h0 in runs:
+                    for e in range(HALVES):
+                        slot_grid = mixers[parity][:, a, e, h0 : h0 + count, :].rearrange(
+                            "q h (r c) -> q h r c", c=MAP_COLS
+                        )
+                        copy(
+                            out=slot_grid[:, :, r_off : r_off + r_len, c_off : c_off + c_len],
+                            in_=bank_grid[:, e, place : place + count, r_off : r_off + r_len, c_in : c_in + c_len],
+                        )
 
         windows_by_half = windows[:].rearrange("q b ww wh (e c) -> q b ww wh e c", e=HALVES)
         unit_banks = {}
@@ -273,22 +293,31 @@ def tile_swinmlpblock_pa_kernel(tc, h_pad, x, sw, sb, g2, b2, w1, bb1, out):
             )
 
         unit_stats = {}
+        unit_mean_var = {}
+        unit_rstd = {}
 
         def statistics(i):
             stats = stage.tile([P, PAIR, STATS], F32)
-            mean_var = stage.tile([P, PAIR, 2], F32)
-            var_eps = stage.tile([P, PAIR], F32)
-            rstd = stage.tile([P, PAIR], F32)
+            unit_stats[i] = stats
             for u in range(PAIR):
                 nc.vector.bn_stats(out=stats[:, u, :], in_=x1[i][:, u, :, :].rearrange("p t c -> p (t c)"))
+
+        def aggregate(i):
+            mean_var = stage.tile([P, PAIR, 2], F32)
+            unit_mean_var[i] = mean_var
             for u in range(PAIR):
-                nc.vector.bn_aggr(out=mean_var[:, u, :], in_=stats[:, u, :])
-            nc.vector.tensor_scalar_add(out=var_eps[:], in0=mean_var[:, :, 1], scalar1=EPS)
+                nc.vector.bn_aggr(out=mean_var[:, u, :], in_=unit_stats[i][:, u, :])
+
+        def invert(i):
+            var_eps = stage.tile([P, PAIR], F32)
+            rstd = stage.tile([P, PAIR], F32)
+            unit_rstd[i] = rstd
+            nc.vector.tensor_scalar_add(out=var_eps[:], in0=unit_mean_var[i][:, :, 1], scalar1=EPS)
             nc.gpsimd.tensor_tensor(out=rstd[:], in0=var_eps[:], in1=minus_half[:], op=ALU.pow)
-            unit_stats[i] = (mean_var, rstd)
 
         def normalise(engine, i):
-            mean_var, rstd = unit_stats[i]
+            mean_var = unit_mean_var[i]
+            rstd = unit_rstd[i]
             for u in range(PAIR):
                 engine.tensor_scalar(
                     out=x1[i][:, u, :, :],
@@ -408,32 +437,39 @@ def tile_swinmlpblock_pa_kernel(tc, h_pad, x, sw, sb, g2, b2, w1, bb1, out):
             widen_gain()
             spread_bias(0)
             spread_bias(1)
+            keep_bias(sc, 0)
+            keep_bias(sc, 1)
             regroup_w1(sc, 0)
             add_x(0, 0)
             add_x(0, 1)
             statistics(0)
+            aggregate(0)
+            invert(0)
+            for a in range(2, 4):
+                clear(nc.gpsimd, second, a)
             mix_open(1)
-            for a in range(2):
-                for k in range(2):
-                    mix_patch(1, k, a)
-            keep_bias(ve, 0)
+            for k in range(2):
+                mix_patch(1, k, 0)
+            regroup_w1(ve, 1)
             normalise(nc.vector, 0)
             flip_h2(0)
-            regroup_w1(ve, 1)
+            for k in range(2):
+                mix_patch(1, k, 1)
+            quantise_w1(0)
             add_x(1, 0)
             add_x(1, 1)
-            quantise_w1(0)
-            flip_sw(second, 0)
             statistics(1)
+            flip_sw(second, 0)
+            aggregate(1)
             keep_sw(second, 0, sc)
             flip_sw(second, 1)
-            quantise_w1(1)
             regroup_h2(0)
+            invert(1)
+            quantise_w1(1)
             keep_sw(second, 1, sc)
             mix_open(2)
             for a in range(2):
                 mix_patch(2, 0, a)
-            keep_bias(ve, 1)
             quantise_h2(0)
             normalise(nc.vector, 1)
             multiply(0, 0, 0)
@@ -475,6 +511,8 @@ def tile_swinmlpblock_pa_kernel(tc, h_pad, x, sw, sb, g2, b2, w1, bb1, out):
             for a in range(2):
                 mix_patch(3, 0, a)
             statistics(2)
+            aggregate(2)
+            invert(2)
             multiply(0, 1, 3)
             multiply(1, 0, 3)
             finish(0, 0, 3)
@@ -500,6 +538,8 @@ def tile_swinmlpblock_pa_kernel(tc, h_pad, x, sw, sb, g2, b2, w1, bb1, out):
             quantise_h2(2)
             add_x(3, 1)
             statistics(3)
+            aggregate(3)
+            invert(3)
             multiply(2, 0, 0)
             finish(1, 1, 2)
             multiply(2, 0, 1)

@@ -186,7 +186,7 @@ def tile_swinmlpblock_pa_kernel(tc, h_pad, x, sw, sb, g2, b2, w1, bb1, out):
 
         clear(nc.vector, first, 0)
         clear(nc.gpsimd, first, 1)
-        for a in range(2):
+        for a in range(len(patches[second])):
             clear(nc.gpsimd, second, a)
 
         gain_bias = const.tile([P, 2 * PACK], F32)
@@ -280,15 +280,14 @@ def tile_swinmlpblock_pa_kernel(tc, h_pad, x, sw, sb, g2, b2, w1, bb1, out):
                         stop=((a, hh, e) == last),
                     )
 
-        x1 = [keep.tile([P, PAIR, PACK, P], F32, name="x1_%d" % i) for i in range(len(units))]
+        x1 = [keep.tile([P, PAIR, CH], F32, name="x1_%d" % i) for i in range(len(units))]
 
         def add_x(i, k):
             channels = slice(BANK_CH * k, BANK_CH * (k + 1))
-            columns = slice(BANK_CH // PACK * k, BANK_CH // PACK * (k + 1))
             nc.vector.tensor_tensor(
-                out=x1[i][:, :, :, columns].rearrange("p u t (h c) -> p u h c t", h=MIX_HEADS),
-                in0=unit_banks[(i, k)][:].rearrange("p h (u c t) -> p u h c t", u=PAIR, t=PACK),
-                in1=x_tiles[i][:, :, channels].rearrange("p u (h c t) -> p u h c t", h=MIX_HEADS, t=PACK),
+                out=x1[i][:, :, channels].rearrange("p u (h d) -> p u h d", d=HEAD_CH),
+                in0=unit_banks[(i, k)][:].rearrange("p h (u d) -> p u h d", u=PAIR),
+                in1=x_tiles[i][:, :, channels].rearrange("p u (h d) -> p u h d", d=HEAD_CH),
                 op=ALU.add,
             )
 
@@ -300,7 +299,7 @@ def tile_swinmlpblock_pa_kernel(tc, h_pad, x, sw, sb, g2, b2, w1, bb1, out):
             stats = stage.tile([P, PAIR, STATS], F32)
             unit_stats[i] = stats
             for u in range(PAIR):
-                nc.vector.bn_stats(out=stats[:, u, :], in_=x1[i][:, u, :, :].rearrange("p t c -> p (t c)"))
+                nc.vector.bn_stats(out=stats[:, u, :], in_=x1[i][:, u, :])
 
         def aggregate(i):
             mean_var = stage.tile([P, PAIR, 2], F32)
@@ -315,13 +314,15 @@ def tile_swinmlpblock_pa_kernel(tc, h_pad, x, sw, sb, g2, b2, w1, bb1, out):
             nc.vector.tensor_scalar_add(out=var_eps[:], in0=unit_mean_var[i][:, :, 1], scalar1=EPS)
             nc.gpsimd.tensor_tensor(out=rstd[:], in0=var_eps[:], in1=minus_half[:], op=ALU.pow)
 
-        def normalise(engine, i):
+        normed = [keep.tile([P, PAIR, PACK, P], F32, name="normed%d" % s) for s in range(2)]
+
+        def normalise(i):
             mean_var = unit_mean_var[i]
             rstd = unit_rstd[i]
             for u in range(PAIR):
-                engine.tensor_scalar(
-                    out=x1[i][:, u, :, :],
-                    in0=x1[i][:, u, :, :],
+                nc.vector.tensor_scalar(
+                    out=normed[i % 2][:, u, :, :].rearrange("s t p -> s p t"),
+                    in0=x1[i][:, u, :].rearrange("s (p t) -> s p t", t=PACK),
                     scalar1=mean_var[:, u, 0:1],
                     scalar2=rstd[:, u : u + 1],
                     op0=ALU.subtract,
@@ -335,7 +336,7 @@ def tile_swinmlpblock_pa_kernel(tc, h_pad, x, sw, sb, g2, b2, w1, bb1, out):
                 bank = flip_banks.tile([P, 2, PAIR, P], F32, tag="flip")
                 for u in range(PAIR):
                     for tt in range(2):
-                        nc.tensor.transpose(bank[:, tt, u, :], x1[i][:, u, t0 + tt, :], ident_f32[:])
+                        nc.tensor.transpose(bank[:, tt, u, :], normed[i % 2][:, u, t0 + tt, :], ident_f32[:])
                 for tt in range(2):
                     t = t0 + tt
                     nc.scalar.activation(
@@ -445,13 +446,11 @@ def tile_swinmlpblock_pa_kernel(tc, h_pad, x, sw, sb, g2, b2, w1, bb1, out):
             statistics(0)
             aggregate(0)
             invert(0)
-            for a in range(2, 4):
-                clear(nc.gpsimd, second, a)
             mix_open(1)
             for k in range(2):
                 mix_patch(1, k, 0)
             regroup_w1(ve, 1)
-            normalise(nc.vector, 0)
+            normalise(0)
             flip_h2(0)
             for k in range(2):
                 mix_patch(1, k, 1)
@@ -471,7 +470,7 @@ def tile_swinmlpblock_pa_kernel(tc, h_pad, x, sw, sb, g2, b2, w1, bb1, out):
             for a in range(2):
                 mix_patch(2, 0, a)
             quantise_h2(0)
-            normalise(nc.vector, 1)
+            normalise(1)
             multiply(0, 0, 0)
             multiply(0, 0, 1)
             flip_h2(1)
@@ -520,7 +519,7 @@ def tile_swinmlpblock_pa_kernel(tc, h_pad, x, sw, sb, g2, b2, w1, bb1, out):
                 mix_patch(3, 0, a)
             finish(0, 1, 3)
             quantise_w1(2)
-            normalise(nc.vector, 2)
+            normalise(2)
             multiply(0, 0, 2)
             multiply(0, 1, 2)
             flip_h2(2)
@@ -546,7 +545,7 @@ def tile_swinmlpblock_pa_kernel(tc, h_pad, x, sw, sb, g2, b2, w1, bb1, out):
             finish(1, 1, 3)
             multiply(2, 0, 2)
             finish(2, 0, 0)
-            normalise(nc.vector, 3)
+            normalise(3)
             flip_h2(3)
             finish(2, 0, 1)
             multiply(2, 0, 3)

from contextlib import ExitStack

import concourse.mybir as mybir
from concourse.masks import make_identity

BF16 = mybir.dt.bfloat16
F32 = mybir.dt.float32
U32 = mybir.dt.uint32
U8 = mybir.dt.uint8
FP8X4 = mybir.dt.float8_e4m3fn_x4
ACT = mybir.ActivationFunctionType
ALU = mybir.AluOpType

P = 128
BATCH = 2
MAP_ROWS = 32
MAP_COLS = 16
CH = 512
HEADS = 16
WS = 16
SHIFT = 7
HID = 2048
HEAD_CH = CH // HEADS
POSITIONS = WS * WS
PAD = WS - SHIFT
WINDOWS_DOWN = (MAP_ROWS + WS) // WS
WINDOWS_ACROSS = (MAP_COLS + WS) // WS
EPS = 1e-5

TILE_ROWS = P // MAP_COLS
PARITIES = 2
PAIR = MAP_ROWS // TILE_ROWS // PARITIES
HALVES = 2
PACK = 4
FLIP_HEADS = 4
MIX_HEADS = 8
MIX_BANKS = HEADS // MIX_HEADS
BANK_CH = MIX_HEADS * HEAD_CH
BF16_BLOCKS_PER_BANK = 8
N_MX = 512
HID_CHUNKS = HID // N_MX
STATS = 6
STORE_HALVES = 2
HALF_HID = HID // STORE_HALVES
CHUNKS_PER_HALF = HID_CHUNKS // STORE_HALVES

FLOPS = (
    2 * HEADS * POSITIONS * POSITIONS * BATCH * WINDOWS_DOWN * WINDOWS_ACROSS * HEAD_CH
    + 2 * BATCH * MAP_ROWS * MAP_COLS * CH * HID
)


def pieces_by_window(first, count):
    pieces = []
    offset = 0
    while offset < count:
        window, inside = divmod(first + offset, WS)
        length = min(count - offset, WS - inside)
        pieces.append((offset, length, inside, window))
        offset += length
    return pieces


def tile_swinmlpblock_pa_kernel(tc, h_pad, x, sw, sb, g2, b2, w1, bb1, out):
    nc = tc.nc

    row_pieces = [pieces_by_window(PAD + TILE_ROWS * parity, TILE_ROWS) for parity in range(PARITIES)]
    col_pieces = pieces_by_window(PAD, MAP_COLS)
    patches = [[(rp, cp) for rp in reversed(row_pieces[parity]) for cp in col_pieces] for parity in range(PARITIES)]
    first, second = 1, 0
    units = [(parity, b) for parity in (first, second) for b in range(BATCH)]

    with ExitStack() as stack:
        const = stack.enter_context(tc.tile_pool(name="const", bufs=1))
        keep = stack.enter_context(tc.tile_pool(name="keep", bufs=1))
        stage = stack.enter_context(tc.tile_pool(name="stage", bufs=2))
        results = stack.enter_context(tc.tile_pool(name="results", bufs=8))
        flip_banks = stack.enter_context(tc.psum_pool(name="flip_banks", bufs=3))
        mix_banks = stack.enter_context(tc.psum_pool(name="mix_banks", bufs=2))
        mx_banks = stack.enter_context(tc.psum_pool(name="mx_banks", bufs=3))

        sw_rows = [keep.tile([P, HEADS, POSITIONS], BF16, name="sw_rows%d" % s) for s in range(PARITIES)]
        mixers = [
            keep.tile([P, len(patches[s]), HALVES, HEADS, P], BF16, name="mixers%d" % s) for s in range(PARITIES)
        ]
        windows = keep.tile([P, BATCH, WINDOWS_ACROSS, WINDOWS_DOWN, HALVES * CH], BF16)
        x_tiles = [keep.tile([P, PAIR, CH], BF16, name="x_tiles%d" % i) for i in range(len(units))]
        w1_raw = [keep.tile([P, PACK, HALF_HID], BF16, name="w1_raw%d" % i) for i in range(STORE_HALVES)]
        w1_codes = keep.tile([P, HID], U32, align_bytes=64)
        w1_scales = keep.tile([P, HID], U8, align_bytes=64)
        h2_codes = keep.tile([P, len(units), PAIR * P], U32, align_bytes=64)
        h2_scales = keep.tile([P, len(units), PAIR * P], U8, align_bytes=64)
        bias_rows = const.tile([P, HID], BF16)

        bias_raw = const.tile([P, P], BF16)
        sb_raw = const.tile([HEADS, POSITIONS], BF16)
        gain_raw = const.tile([P, PACK], BF16)
        shift_raw = const.tile([P, PACK], BF16)
        nc.vector.memset(bias_raw[:], 0.0)
        nc.scalar.dma_start(out=sb_raw[:], in_=sb)
        nc.scalar.dma_start(out=bias_raw[0 : HID // P, :], in_=bb1.rearrange("(m p) -> m p", p=P))
        nc.scalar.dma_start(out=gain_raw[:], in_=g2.rearrange("(p t) -> p t", t=PACK))
        nc.scalar.dma_start(out=shift_raw[:], in_=b2.rearrange("(p t) -> p t", t=PACK))

        sw_by_row = sw.rearrange("h i j -> i h j")
        sw_start = WS * row_pieces[second][0][2]
        sw_shifted = sw.flatten_outer_dims()[sw_start : sw_start + POSITIONS * (HEADS - 1), :].rearrange(
            "(h i) j -> i h j", i=POSITIONS
        )
        window_view = h_pad.rearrange(
            "b (wh r) (ww q e) c -> b wh ww r q (e c)", r=WS, ww=WINDOWS_ACROSS, e=HALVES
        )
        x_view = x.flatten_outer_dims().rearrange("(b u s p) c -> s b p u c", b=BATCH, u=PAIR, p=P)
        w1_view = w1.rearrange("(p t) n -> p t n", t=PACK)
        out_rows = out.flatten_outer_dims()

        def load_sw_rows(parity):
            (offset, length, inside, window), wrapped = row_pieces[parity][0], row_pieces[parity][1:]
            split = WS * length
            if wrapped:
                nc.sync.dma_start(out=sw_rows[parity][0:split, 0, :], in_=sw[HEADS - 1, POSITIONS - split : POSITIONS, :])
                nc.sync.dma_start(out=sw_rows[parity][split:P, 0, :], in_=sw[0, 0 : P - split, :])
            for g0 in range(0, HEADS, FLIP_HEADS):
                first_place = max(g0, len(wrapped))
                places = slice(first_place, g0 + FLIP_HEADS)
                heads = slice(first_place - len(wrapped), g0 + FLIP_HEADS - len(wrapped))
                nc.sync.dma_start(
                    out=sw_rows[parity][:, places, :],
                    in_=sw_by_row[WS * inside : WS * inside + P, heads, :]
                    if not wrapped
                    else sw_shifted[0:P, heads, :],
                )

        def load_windows(b, rows):
            for ww in range(WINDOWS_ACROSS):
                for wh in rows:
                    nc.sync.dma_start(out=windows[:, b, ww, wh, :], in_=window_view[b, wh, ww])

        def load_x(i):
            parity, b = units[i]
            nc.sync.dma_start(out=x_tiles[i][:], in_=x_view[parity, b])

        def load_w1(half):
            nc.sync.dma_start(out=w1_raw[half][:], in_=w1_view[:, :, HALF_HID * half : HALF_HID * (half + 1)])

        load_sw_rows(first)
        load_windows(0, (1, 2))
        load_x(0)
        load_w1(0)
        load_windows(1, (1, 2))
        load_x(1)
        load_sw_rows(second)
        load_w1(1)
        load_windows(0, (0,))
        load_x(2)
        load_windows(1, (0,))
        load_x(3)

        ident_bf = const.tile([P, P], BF16)
        ident_f32 = const.tile([P, P], F32)
        minus_half = const.tile([P, PAIR], F32)
        nc.gpsimd.memset(minus_half[:], -0.5)
        make_identity(nc, ident_f32[:])
        make_identity(nc, ident_bf[:])

        warm = const.tile([P, 1], F32)
        nc.scalar.activation(out=warm[:], in_=minus_half[:, 0:1], func=ACT.Gelu)

        sb_rows = const.tile([P, PARITIES, P], BF16)
        nc.vector.memset(sb_rows[:], 0.0)
        sb_grid = sb_raw[:].rearrange("h (r c) -> h r c", c=WS)
        for parity in range(PARITIES):
            slot_grid = sb_rows[0:HEADS, parity, :].rearrange("h (r c) -> h r c", c=MAP_COLS)
            for (r_off, r_len, r_in, r_win), (c_off, c_len, c_in, c_win) in patches[parity]:
                nc.scalar.copy(
                    out=slot_grid[:, r_off : r_off + r_len, c_off : c_off + c_len],
                    in_=sb_grid[:, r_in : r_in + r_len, c_in : c_in + c_len],
                )
        pick_head = const.tile([P, HEADS, PAIR * HEAD_CH], BF16)
        nc.scalar.copy(
            out=pick_head[:], in_=ident_bf[:, 0:HEADS].unsqueeze(2).to_broadcast([P, HEADS, PAIR * HEAD_CH])
        )

        def clear(engine, parity, patch):
            engine.memset(mixers[parity][:, patch, :, :, :].rearrange("q e h m -> q (e h m)").bitcast(F32), 0.0)

        clear(nc.vector, first, 0)
        clear(nc.gpsimd, first, 1)
        for a in range(len(patches[second])):
            clear(nc.gpsimd, second, a)

        gain_bias = const.tile([P, 2 * PACK], F32)
        bias_columns = const.tile([P, HID // P], BF16)

        def flip_bias():
            bias_flipped = mx_banks.tile([P, BF16_BLOCKS_PER_BANK, P], BF16, tag="bank")
            nc.tensor.transpose(bias_flipped[:, 0, :], bias_raw[:], ident_bf[:])
            nc.vector.tensor_copy(out=bias_columns[:], in_=bias_flipped[:, 0, 0 : HID // P])

        bias_banks = {}

        def spread_bias(half):
            bank = mx_banks.tile([P, BF16_BLOCKS_PER_BANK, P], BF16, tag="bank")
            bias_banks[half] = bank
            m0 = BF16_BLOCKS_PER_BANK * half
            for mm in range(BF16_BLOCKS_PER_BANK):
                nc.tensor.transpose(
                    bank[:, mm, :], bias_columns[:, m0 + mm : m0 + mm + 1].to_broadcast([P, P]), ident_bf[:]
                )

        def keep_bias(copy, half):
            copy(
                out=bias_rows[:, HALF_HID * half : HALF_HID * (half + 1)],
                in_=bias_banks[half][:].rearrange("p m i -> p (m i)"),
            )

        def widen_gain():
            nc.vector.tensor_copy(out=gain_bias[:, 0:PACK], in_=gain_raw[:])
            nc.vector.tensor_copy(out=gain_bias[:, PACK : 2 * PACK], in_=shift_raw[:])

        sw_banks = {}

        def flip_sw(parity, k):
            sw_words = sw_rows[parity][:].bitcast(F32)
            bank = flip_banks.tile([P, FLIP_HEADS, P], F32, tag="flip")
            sw_banks[(parity, k)] = bank
            for hh in range(FLIP_HEADS):
                nc.tensor.transpose(bank[:, hh, :], sw_words[:, FLIP_HEADS * k + hh, :], ident_f32[:])

        def keep_sw(parity, k, copy):
            g0 = FLIP_HEADS * k
            bank = sw_banks[(parity, k)]
            bank_grid = bank[:].bitcast(BF16).rearrange("q h (r c e) -> q e h r c", c=WS, e=HALVES)
            for a, ((r_off, r_len, r_in, r_win), (c_off, c_len, c_in, c_win)) in enumerate(patches[parity]):
                if len(row_pieces[parity]) == 1 or r_off > 0:
                    runs = [(0, FLIP_HEADS, g0)]
                elif g0 == 0:
                    runs = [(0, 1, HEADS - 1), (1, FLIP_HEADS - 1, 0)]
                else:
                    runs = [(0, FLIP_HEADS, g0 - 1)]
                for place, count, h0 in runs:
                    for e in range(HALVES):
                        slot_grid = mixers[parity][:, a, e, h0 : h0 + count, :].rearrange(
                            "q h (r c) -> q h r c", c=MAP_COLS
                        )
                        copy(
                            out=slot_grid[:, :, r_off : r_off + r_len, c_off : c_off + c_len],
                            in_=bank_grid[:, e, place : place + count, r_off : r_off + r_len, c_in : c_in + c_len],
                        )

        windows_by_half = windows[:].rearrange("q b ww wh (e c) -> q b ww wh e c", e=HALVES)
        unit_banks = {}

        def mix_open(i):
            parity, b = units[i]
            for k in range(MIX_BANKS):
                bank = mix_banks.tile([P, MIX_HEADS, PAIR * HEAD_CH], F32, tag="mix")
                unit_banks[(i, k)] = bank
                nc.tensor.matmul(
                    bank[:].rearrange("p h n -> p (h n)"),
                    lhsT=sb_rows[:, parity, :],
                    rhs=pick_head[:, MIX_HEADS * k : MIX_HEADS * (k + 1), :].rearrange("k h n -> k (h n)"),
                    start=True,
                    stop=False,
                )

        def mix_patch(i, k, a):
            parity, b = units[i]
            bank = unit_banks[(i, k)]
            (r_off, r_len, r_in, r_win), (c_off, c_len, c_in, c_win) = patches[parity][a]
            last = (len(patches[parity]) - 1, MIX_HEADS - 1, HALVES - 1)
            for hh in range(MIX_HEADS):
                h = MIX_HEADS * k + hh
                for e in range(HALVES):
                    nc.tensor.matmul(
                        bank[:, hh, :].rearrange("p (u d) -> p u d", d=HEAD_CH),
                        lhsT=mixers[parity][:, a, e, h, :],
                        rhs=windows_by_half[:, b, c_win, r_win : r_win + PAIR, e, HEAD_CH * h : HEAD_CH * (h + 1)],
                        start=False,
                        stop=((a, hh, e) == last),
                    )

        x1 = [keep.tile([P, PAIR, CH], F32, name="x1_%d" % i) for i in range(len(units))]

        def add_x(i, k):
            channels = slice(BANK_CH * k, BANK_CH * (k + 1))
            nc.vector.tensor_tensor(
                out=x1[i][:, :, channels].rearrange("p u (h d) -> p u h d", d=HEAD_CH),
                in0=unit_banks[(i, k)][:].rearrange("p h (u d) -> p u h d", u=PAIR),
                in1=x_tiles[i][:, :, channels].rearrange("p u (h d) -> p u h d", d=HEAD_CH),
                op=ALU.add,
            )

        unit_stats = {}
        unit_mean_var = {}
        unit_rstd = {}

        def statistics(i):
            stats = stage.tile([P, PAIR, STATS], F32)
            unit_stats[i] = stats
            for u in range(PAIR):
                nc.vector.bn_stats(out=stats[:, u, :], in_=x1[i][:, u, :])

        def aggregate(i):
            mean_var = stage.tile([P, PAIR, 2], F32)
            unit_mean_var[i] = mean_var
            for u in range(PAIR):
                nc.vector.bn_aggr(out=mean_var[:, u, :], in_=unit_stats[i][:, u, :])

        def invert(i):
            var_eps = stage.tile([P, PAIR], F32)
            rstd = stage.tile([P, PAIR], F32)
            unit_rstd[i] = rstd
            nc.vector.tensor_scalar_add(out=var_eps[:], in0=unit_mean_var[i][:, :, 1], scalar1=EPS)
            nc.gpsimd.tensor_tensor(out=rstd[:], in0=var_eps[:], in1=minus_half[:], op=ALU.pow)

        normed = [keep.tile([P, PAIR, PACK, P], F32, name="normed%d" % s) for s in range(2)]

        def normalise(i):
            mean_var = unit_mean_var[i]
            rstd = unit_rstd[i]
            for u in range(PAIR):
                nc.vector.tensor_scalar(
                    out=normed[i % 2][:, u, :, :].rearrange("s t p -> s p t"),
                    in0=x1[i][:, u, :].rearrange("s (p t) -> s p t", t=PACK),
                    scalar1=mean_var[:, u, 0:1],
                    scalar2=rstd[:, u : u + 1],
                    op0=ALU.subtract,
                    op1=ALU.mult,
                )

        planes = [keep.tile([P, PACK, PAIR * P], BF16, name="planes%d" % s) for s in range(2)]

        def flip_h2(i):
            for t0 in range(0, PACK, 2):
                bank = flip_banks.tile([P, 2, PAIR, P], F32, tag="flip")
                for u in range(PAIR):
                    for tt in range(2):
                        nc.tensor.transpose(bank[:, tt, u, :], normed[i % 2][:, u, t0 + tt, :], ident_f32[:])
                for tt in range(2):
                    t = t0 + tt
                    nc.scalar.activation(
                        out=planes[i % 2][:, t, :],
                        in_=bank[:, tt, :, :].rearrange("p u m -> p (u m)"),
                        func=ACT.Identity,
                        scale=gain_bias[:, t : t + 1],
                        bias=gain_bias[:, PACK + t : PACK + t + 1],
                    )

        def regroup(copy, dst, src):
            copy(out=dst.rearrange("p (n i) t -> p n t i", i=4), in_=src.rearrange("p t (n i) -> p n t i", i=4))

        h2_words = [keep.tile([P, PAIR * P, PACK], BF16, align_bytes=64, name="h2_words%d" % s) for s in range(2)]

        def regroup_h2(i):
            regroup(nc.vector.tensor_copy, h2_words[i % 2][:], planes[i % 2][:])

        def quantise_h2(i):
            nc.vector.quantize_mx(
                out=h2_codes[:, i, :].bitcast(FP8X4),
                scales=h2_scales[:, i, :],
                in_=h2_words[i % 2][:].rearrange("p n t -> p (n t)"),
            )

        w1_words = keep.tile([P, HID_CHUNKS, N_MX, PACK], BF16, align_bytes=64)

        def regroup_w1(copy, n):
            half, inside = divmod(n, CHUNKS_PER_HALF)
            regroup(copy, w1_words[:, n, :, :], w1_raw[half][:, :, N_MX * inside : N_MX * (inside + 1)])

        def quantise_w1(n):
            columns = slice(N_MX * n, N_MX * (n + 1))
            nc.vector.quantize_mx(
                out=w1_codes[:, columns].bitcast(FP8X4),
                scales=w1_scales[:, columns],
                in_=w1_words[:, n, :, :].rearrange("p n t -> p (n t)"),
            )

        products = {}
        open_results = {}

        def multiply(i, u, n):
            tokens = slice(P * u, P * (u + 1))
            columns = slice(N_MX * n, N_MX * (n + 1))
            bank = mx_banks.tile([P, N_MX], F32, tag="bank")
            products[(i, u, n)] = bank
            nc.tensor.matmul_mx(
                out=bank[:],
                lhsT=h2_codes[:, i, tokens].bitcast(FP8X4),
                lhsT_scale=h2_scales[:, i, tokens],
                rhs=w1_codes[:, columns].bitcast(FP8X4),
                rhs_scale=w1_scales[:, columns],
                start=True,
                stop=True,
            )

        def finish(i, u, n):
            parity, b = units[i]
            half, inside = divmod(n, CHUNKS_PER_HALF)
            complete = (i, u, half) in open_results
            if not complete:
                result = results.tile([P, HALF_HID], F32)
                open_results[(i, u, half)] = result
            result = open_results[(i, u, half)]
            columns = slice(N_MX * n, N_MX * (n + 1))
            here = slice(N_MX * inside, N_MX * (inside + 1))
            nc.vector.tensor_tensor(
                out=result[:, here], in0=products[(i, u, n)][:], in1=bias_rows[:, columns], op=ALU.add
            )
            nc.scalar.activation(out=result[:, here], in_=result[:, here], func=ACT.Gelu)
            first_row = P * (PARITIES * (PAIR * b + u) + parity)
            if (i, u, half) == (len(units) - 1, PAIR - 1, STORE_HALVES - 1):
                nc.sync.dma_start(out=out_rows[first_row : first_row + P, columns], in_=result[:, here])
            elif complete:
                nc.sync.dma_start(
                    out=out_rows[first_row : first_row + P, HALF_HID * half : HALF_HID * (half + 1)], in_=result[:]
                )

        def project(i, u, n):
            multiply(i, u, n)
            finish(i, u, n)

        with tc.manual_schedule():
            sc, ve = nc.scalar.copy, nc.vector.tensor_copy
            flip_sw(first, 0)
            flip_sw(first, 1)
            keep_sw(first, 0, ve)
            keep_sw(first, 1, sc)
            flip_sw(first, 2)
            keep_sw(first, 2, ve)
            flip_sw(first, 3)
            keep_sw(first, 3, sc)
            mix_open(0)
            flip_bias()
            for a in range(2):
                for k in range(2):
                    mix_patch(0, k, a)
            widen_gain()
            spread_bias(0)
            spread_bias(1)
            keep_bias(sc, 0)
            keep_bias(sc, 1)
            regroup_w1(sc, 0)
            add_x(0, 0)
            add_x(0, 1)
            statistics(0)
            aggregate(0)
            invert(0)
            mix_open(1)
            for k in range(2):
                mix_patch(1, k, 0)
            regroup_w1(ve, 1)
            normalise(0)
            flip_h2(0)
            for k in range(2):
                mix_patch(1, k, 1)
            quantise_w1(0)
            add_x(1, 0)
            add_x(1, 1)
            statistics(1)
            flip_sw(second, 0)
            aggregate(1)
            keep_sw(second, 0, sc)
            flip_sw(second, 1)
            regroup_h2(0)
            invert(1)
            quantise_w1(1)
            keep_sw(second, 1, sc)
            mix_open(2)
            for a in range(2):
                mix_patch(2, 0, a)
            quantise_h2(0)
            normalise(1)
            multiply(0, 0, 0)
            multiply(0, 0, 1)
            flip_h2(1)
            multiply(0, 1, 0)
            finish(0, 0, 0)
            flip_sw(second, 2)
            keep_sw(second, 2, sc)
            regroup_w1(ve, 3)
            flip_sw(second, 3)
            for a in range(2,4):
                mix_patch(2, 0, a)
            finish(0, 0, 1)
            keep_sw(second, 3, sc)
            multiply(0, 1, 1)
            regroup_h2(1)
            finish(0, 1, 0)
            quantise_w1(3)
            quantise_h2(1)
            finish(0, 1, 1)
            multiply(1, 0, 0)
            multiply(1, 0, 1)
            add_x(2, 0)
            for a in range(2):
                mix_patch(2, 1, a)
            multiply(1, 1, 0)
            finish(1, 0, 0)
            regroup_w1(sc, 2)
            for a in range(2,4):
                mix_patch(2, 1, a)
            finish(1, 0, 1)
            multiply(1, 1, 1)
            multiply(0, 0, 3)
            finish(1, 1, 0)
            add_x(2, 1)
            finish(1, 1, 1)
            mix_open(3)
            for a in range(2):
                mix_patch(3, 0, a)
            statistics(2)
            aggregate(2)
            invert(2)
            multiply(0, 1, 3)
            multiply(1, 0, 3)
            finish(0, 0, 3)
            for a in range(2,4):
                mix_patch(3, 0, a)
            finish(0, 1, 3)
            quantise_w1(2)
            normalise(2)
            multiply(0, 0, 2)
            multiply(0, 1, 2)
            flip_h2(2)
            finish(1, 0, 3)
            add_x(3, 0)
            multiply(1, 0, 2)
            for a in range(4):
                mix_patch(3, 1, a)
            finish(0, 0, 2)
            finish(0, 1, 2)
            multiply(1, 1, 2)
            multiply(1, 1, 3)
            regroup_h2(2)
            finish(1, 0, 2)
            quantise_h2(2)
            add_x(3, 1)
            statistics(3)
            aggregate(3)
            invert(3)
            multiply(2, 0, 0)
            finish(1, 1, 2)
            multiply(2, 0, 1)
            finish(1, 1, 3)
            multiply(2, 0, 2)
            finish(2, 0, 0)
            normalise(3)
            flip_h2(3)
            finish(2, 0, 1)
            multiply(2, 0, 3)
            multiply(2, 1, 0)
            finish(2, 0, 2)
            multiply(2, 1, 1)
            finish(2, 0, 3)
            multiply(2, 1, 2)
            finish(2, 1, 0)
            regroup_h2(3)
            multiply(2, 1, 3)
            finish(2, 1, 1)
            quantise_h2(3)
            finish(2, 1, 2)
            finish(2, 1, 3)
            for u in range(2):
                for n in range(4):
                    project(3, u, n)
